import numpy as np
import ml_dtypes


def mxq(x, axis, fmt="e4m3"):
    dtype, down = {"e4m3": (ml_dtypes.float8_e4m3fn, 7), "e5m2": (ml_dtypes.float8_e5m2, 14)}[fmt]
    v = np.moveaxis(np.asarray(x, np.float32).astype(ml_dtypes.bfloat16).astype(np.float64), axis, -1)
    blocks = v.reshape(v.shape[:-1] + (-1, 32))
    amax = np.abs(blocks).max(-1, keepdims=True)
    byte = np.maximum(np.where(amax > 0, np.frexp(amax)[1] - 1 + 127, 0) - down, 1)
    scale = np.exp2(byte - 127.0)
    codes = (blocks / scale).astype(np.float32).astype(dtype).astype(np.float64)
    return np.moveaxis((codes * scale).reshape(v.shape), -1, axis)


WIDE = False


def mx_kscale(k):
    if not WIDE:
        return np.ones(k)
    levels = np.array([10, -10, 5, -5, 0])
    a = np.random.permutation(np.resize(levels, k // 512 * 4)).reshape(k // 512, 4)
    idx = np.arange(k)
    return np.exp2(a[idx // 512, idx % 128 // 32])


BF16 = ml_dtypes.bfloat16


def bf(x):
    return np.asarray(x, np.float32).astype(BF16)


def f64(x):
    return np.asarray(x).astype(np.float64)


B, T, D, H, QB = 8, 512, 512, 4, 512
DH = D // H


def decay(r0, r1, n):
    gam = 1.0 - 2.0 ** (-5.0 - f64(np.arange(H)))
    diff = f64(np.arange(r0, r1))[:, None] - f64(np.arange(n))[None, :]
    return np.where(diff >= 0, gam[:, None, None] ** np.maximum(diff, 0.0), 0.0)


def heads(z):
    return z.reshape(B, T, H, DH).transpose(0, 2, 1, 3)


def setup_inputs():
    s, t = mx_kscale(D), mx_kscale(T)
    return {"q": bf(np.random.standard_normal((B, T, D))),
            "k": bf(np.random.standard_normal((B, T, D)) * t[:, None]),
            "x": bf(np.random.standard_normal((B, T, D)) * s / t[:, None]),
            "W_v": bf(np.random.standard_normal((D, D)) * 0.3 / np.sqrt(D) / s)}


def reference(q, k, x, W_v):
    qh, kh = heads(f64(q)), heads(f64(k))
    v = mxq(f64(x), 2, "e4m3") @ mxq(f64(W_v), 1, "e4m3").T
    vq = mxq(heads(v), 2, "e4m3")
    y = np.zeros((B, H, T, DH))
    for r0 in range(0, T, QB):
        n = r0 + QB
        qk = qh[:, :, r0:n] @ kh[:, :, :n].transpose(0, 1, 3, 2)
        attn = qk * decay(r0, n, n)[None] / np.sqrt(DH)
        y[:, :, r0:n] = mxq(attn, 3, "e4m3") @ vq[:, :, :n]
    return y.transpose(0, 2, 1, 3).reshape(B, T, D)

@@ -1,0 +1,217 @@
+import math
+from contextlib import ExitStack
+
+import concourse.mybir as mybir
+from concourse.masks import make_identity
+
+F32 = mybir.dt.float32
+BF16 = mybir.dt.bfloat16
+U32 = mybir.dt.uint32
+U8 = mybir.dt.uint8
+FP8X4 = mybir.dt.float8_e4m3fn_x4
+
+P = 128
+PACK = 4
+BATCH = 8
+TOKENS = 512
+CHANNELS = 512
+HEADS = CHANNELS // P
+BLOCKS = TOKENS // P
+ROUNDS = BATCH * HEADS
+OUTPUT_LAG = 3
+
+FLOPS = 3 * 2 * BATCH * TOKENS * TOKENS * CHANNELS
+
+
+def block(n):
+    return slice(P * n, P * (n + 1))
+
+
+def tile_multiscaleretention_pa_t_kernel(tc, q, k, x, W_v, out):
+    nc = tc.nc
+    with ExitStack() as ctx:
+        const = ctx.enter_context(tc.tile_pool(name="const", bufs=1))
+        inputs = ctx.enter_context(tc.tile_pool(name="inputs", bufs=BATCH))
+        per_batch = ctx.enter_context(tc.tile_pool(name="per_batch", bufs=2))
+        per_round = ctx.enter_context(tc.tile_pool(name="per_round", bufs=3))
+        waiting = ctx.enter_context(tc.tile_pool(name="waiting", bufs=OUTPUT_LAG + 1))
+        psum_copy = ctx.enter_context(tc.psum_pool(name="psum_copy", bufs=3))
+        psum_s = ctx.enter_context(tc.psum_pool(name="psum_s", bufs=BLOCKS))
+        psum_y = ctx.enter_context(tc.psum_pool(name="psum_y", bufs=1))
+        ctx.enter_context(tc.manual_schedule())
+
+        def load_rows(pool, matrix, name):
+            rows = pool.tile([P, BLOCKS, CHANNELS], BF16, name=name, tag=name)
+            nc.sync.dma_start(out=rows[:], in_=matrix.rearrange("(r p) c -> p r c", p=P))
+            return rows
+
+        k_sb, q_sb, x_sb = [], [], []
+        k_sb.append(load_rows(inputs, k[0], "k_sb"))
+        q_sb.append(load_rows(inputs, q[0], "q_sb"))
+        w_sb = load_rows(const, W_v, "w_sb")
+        x_sb.append(load_rows(inputs, x[0], "x_sb"))
+        for b in range(1, BATCH):
+            k_sb.append(load_rows(inputs, k[b], "k_sb"))
+            q_sb.append(load_rows(inputs, q[b], "q_sb"))
+            x_sb.append(load_rows(inputs, x[b], "x_sb"))
+
+        far_to_near = dict(pattern=[[1, P], [-P, BLOCKS]], base=P * (BLOCKS - 1), channel_multiplier=-1)
+        distance = const.tile([P, P, BLOCKS], F32, name="distance")
+        nc.gpsimd.iota(distance[:], allow_small_or_imprecise_dtypes=True, **far_to_near)
+        ident_bf16 = const.tile([P, P], BF16, name="ident_bf16")
+        make_identity(nc, ident_bf16[:])
+        ident_f32 = const.tile([P, P], F32, name="ident_f32")
+        make_identity(nc, ident_f32[:])
+
+        decay = []
+        for h in range(HEADS):
+            table = const.tile([P, P, BLOCKS], F32, name="decay_%d" % h)
+            nc.scalar.activation(
+                out=table[:],
+                in_=distance[:],
+                func=mybir.ActivationFunctionType.Exp,
+                scale=math.log(1.0 - 2.0 ** (-5 - h)),
+                bias=-0.5 * math.log(P),
+            )
+            nc.gpsimd.affine_select(
+                out=table[:], in_=table[:], compare_op=mybir.AluOpType.is_ge, fill=0.0, **far_to_near
+            )
+            decay.append(table)
+
+        attn_bf16 = []
+        for n in range(2):
+            zeroed = const.tile([P, TOKENS, PACK], BF16, name="attn_bf16_%d" % n, align_bytes=64)
+            nc.vector.memset(zeroed[:], 0.0)
+            attn_bf16.append(zeroed)
+
+        def channels_to_partitions(rows, pool, name):
+            grouped = pool.tile([P, TOKENS * PACK], BF16, name=name, align_bytes=64)
+            pairs = grouped[:].bitcast(F32).rearrange("p (n u) -> p n u", u=2)
+            for half in range(2):
+                bank = psum_copy.tile([P, 2, 2 * P], F32, name="pairs_ps", tag="copy")
+                for r in range(2):
+                    row_pairs = rows[:, 2 * half + r, :].bitcast(F32)
+                    for u in range(2):
+                        nc.tensor.transpose(bank[:, u, block(r)], row_pairs[:, block(u)], ident_f32[:])
+                nc.scalar.copy(
+                    out=pairs[:, 2 * P * half : 2 * P * (half + 1), :],
+                    in_=bank[:].rearrange("p u n -> p n u"),
+                )
+            return grouped
+
+        def quantise(grouped, pool, name):
+            words = pool.tile([P, TOKENS], U32, name=name + "_words", align_bytes=64)
+            scales = pool.tile([P, TOKENS], U8, name=name + "_scales", align_bytes=64)
+            nc.vector.quantize_mx(out=words[:].bitcast(FP8X4), scales=scales[:], in_=grouped)
+            return words, scales
+
+        x_bf16, x_mx, v_bf16, v_mx = {}, {}, {}, {}
+
+        def project_values(b, heads):
+            for h in heads:
+                v_ps = psum_copy.tile([P, BLOCKS, P], F32, name="v_ps", tag="copy")
+                for j in range(BLOCKS):
+                    nc.tensor.matmul_mx(
+                        out=v_ps[:, j, :],
+                        lhsT=x_mx[b][0][:, block(j)].bitcast(FP8X4),
+                        lhsT_scale=x_mx[b][1][:, block(j)],
+                        rhs=w_mx[0][:, block(h)].bitcast(FP8X4),
+                        rhs_scale=w_mx[1][:, block(h)],
+                        start=True,
+                        stop=True,
+                    )
+                nc.scalar.copy(out=v_bf16[b][:, h, :, :], in_=v_ps[:].rearrange("p j c -> p c j"))
+
+        kq, s_ps, a_mx = {}, {}, {}
+
+        def head_channels_to_partitions(r):
+            if r >= ROUNDS:
+                return
+            b, h = divmod(r, HEADS)
+            kq_ps = psum_copy.tile([P, 2, TOKENS], BF16, name="kq_ps", tag="copy")
+            for n in range(BLOCKS):
+                nc.tensor.transpose(kq_ps[:, 0, block(n)], k_sb[b][:, n, block(h)], ident_bf16[:])
+            for n in range(BLOCKS):
+                nc.tensor.transpose(kq_ps[:, 1, block(n)], q_sb[b][:, n, block(h)], ident_bf16[:])
+            kq[r] = per_round.tile([P, 2, TOKENS], BF16, name="kq")
+            nc.scalar.copy(out=kq[r][:], in_=kq_ps[:])
+
+        def scores(r, i):
+            if r >= ROUNDS:
+                return
+            s_ps[i] = psum_s.tile([P, BLOCKS, P], F32, name="s_ps")
+            for j in range(i + 1):
+                nc.tensor.matmul(
+                    out=s_ps[i][:, j, :],
+                    lhsT=kq[r][:, 0, block(j)],
+                    rhs=kq[r][:, 1, block(i)],
+                    start=True,
+                    stop=True,
+                )
+
+        def apply_decay(r, i):
+            nc.vector.tensor_tensor(
+                out=attn_bf16[r % 2][:, block(i), 0 : i + 1],
+                in0=s_ps[i][:, 0 : i + 1, :].rearrange("p j t -> p t j"),
+                in1=decay[r % HEADS][:, :, BLOCKS - 1 - i : BLOCKS],
+                op=mybir.AluOpType.mult,
+            )
+
+        def quantise_attn(r):
+            if r >= 0:
+                a_mx[r] = quantise(attn_bf16[r % 2][:].rearrange("p t j -> p (t j)"), waiting, "a")
+
+        def output(r):
+            if r < 0:
+                return
+            b, h = divmod(r, HEADS)
+            y_ps = psum_y.tile([P, BLOCKS, P], F32, name="y_ps")
+            for i in range(BLOCKS):
+                nc.tensor.matmul_mx(
+                    out=y_ps[:, i, :],
+                    lhsT=a_mx[r][0][:, block(i)].bitcast(FP8X4),
+                    lhsT_scale=a_mx[r][1][:, block(i)],
+                    rhs=v_mx[b][0][:, block(h)].bitcast(FP8X4),
+                    rhs_scale=v_mx[b][1][:, block(h)],
+                    start=True,
+                    stop=True,
+                )
+            y_sb = per_round.tile([P, BLOCKS, P], F32, name="y_sb")
+            nc.scalar.copy(out=y_sb[:], in_=y_ps[:])
+            nc.scalar.dma_start(
+                out=out[b][:, block(h)].rearrange("(i p) c -> p i c", p=P), in_=y_sb[:]
+            )
+
+        def head_round(r):
+            apply_decay(r, 0)
+            scores(r + 1, 0)
+            quantise_attn(r - 1)
+            head_channels_to_partitions(r + 2)
+            output(r - OUTPUT_LAG)
+            for i in range(1, BLOCKS):
+                apply_decay(r, i)
+                scores(r + 1, i)
+
+        head_channels_to_partitions(0)
+        head_channels_to_partitions(1)
+        for i in range(BLOCKS):
+            scores(0, i)
+        w_bf16 = channels_to_partitions(w_sb, const, "w_bf16")
+        x_bf16[0] = channels_to_partitions(x_sb[0], per_batch, "x_bf16")
+        for b in range(BATCH):
+            head_round(HEADS * b)
+            if b == 0:
+                w_mx = quantise(w_bf16[:], const, "w")
+            x_mx[b] = quantise(x_bf16[b][:], per_batch, "x")
+            v_bf16[b] = per_batch.tile([P, HEADS, P, PACK], BF16, name="v_bf16", align_bytes=64)
+            project_values(b, (0, 1))
+            head_round(HEADS * b + 1)
+            project_values(b, (2, 3))
+            head_round(HEADS * b + 2)
+            v_mx[b] = quantise(v_bf16[b][:].rearrange("p h c j -> p (h c j)"), per_batch, "v")
+            head_round(HEADS * b + 3)
+            if b + 1 < BATCH:
+                x_bf16[b + 1] = channels_to_partitions(x_sb[b + 1], per_batch, "x_bf16")
+        quantise_attn(ROUNDS - 1)
+        for r in range(ROUNDS - OUTPUT_LAG, ROUNDS):
+            output(r)

@@ -35,9 +35,8 @@ def tile_multiscaleretention_pa_t_kernel(tc, q, k, x, W_v, out):
         per_batch = ctx.enter_context(tc.tile_pool(name="per_batch", bufs=2))
         per_round = ctx.enter_context(tc.tile_pool(name="per_round", bufs=3))
         waiting = ctx.enter_context(tc.tile_pool(name="waiting", bufs=OUTPUT_LAG + 1))
-        psum_copy = ctx.enter_context(tc.psum_pool(name="psum_copy", bufs=3))
+        psum_copy = ctx.enter_context(tc.psum_pool(name="psum_copy", bufs=4))
         psum_s = ctx.enter_context(tc.psum_pool(name="psum_s", bufs=BLOCKS))
-        psum_y = ctx.enter_context(tc.psum_pool(name="psum_y", bufs=1))
         ctx.enter_context(tc.manual_schedule())
 
         def load_rows(pool, matrix, name):
@@ -165,7 +164,7 @@ def tile_multiscaleretention_pa_t_kernel(tc, q, k, x, W_v, out):
             if r < 0:
                 return
             b, h = divmod(r, HEADS)
-            y_ps = psum_y.tile([P, BLOCKS, P], F32, name="y_ps")
+            y_ps = psum_copy.tile([P, BLOCKS, P], F32, name="y_ps", tag="copy")
             for i in range(BLOCKS):
                 nc.tensor.matmul_mx(
                     out=y_ps[:, i, :],
@@ -186,11 +185,14 @@ def tile_multiscaleretention_pa_t_kernel(tc, q, k, x, W_v, out):
             apply_decay(r, 0)
             scores(r + 1, 0)
             quantise_attn(r - 1)
-            head_channels_to_partitions(r + 2)
             output(r - OUTPUT_LAG)
-            for i in range(1, BLOCKS):
-                apply_decay(r, i)
-                scores(r + 1, i)
+            apply_decay(r, 1)
+            scores(r + 1, 1)
+            head_channels_to_partitions(r + 2)
+            apply_decay(r, 2)
+            scores(r + 1, 2)
+            apply_decay(r, 3)
+            scores(r + 1, 3)
 
         head_channels_to_partitions(0)
         head_channels_to_partitions(1)
@@ -198,20 +200,26 @@ def tile_multiscaleretention_pa_t_kernel(tc, q, k, x, W_v, out):
             scores(0, i)
         w_bf16 = channels_to_partitions(w_sb, const, "w_bf16")
         x_bf16[0] = channels_to_partitions(x_sb[0], per_batch, "x_bf16")
+
+        def start_projection(b):
+            x_mx[b] = quantise(x_bf16[b][:], per_batch, "x")
+            v_bf16[b] = per_batch.tile([P, HEADS, P, PACK], BF16, name="v_bf16", align_bytes=64)
+            project_values(b, (0, 1))
+
         for b in range(BATCH):
             head_round(HEADS * b)
             if b == 0:
                 w_mx = quantise(w_bf16[:], const, "w")
-            x_mx[b] = quantise(x_bf16[b][:], per_batch, "x")
-            v_bf16[b] = per_batch.tile([P, HEADS, P, PACK], BF16, name="v_bf16", align_bytes=64)
-            project_values(b, (0, 1))
-            head_round(HEADS * b + 1)
+                start_projection(0)
             project_values(b, (2, 3))
+            head_round(HEADS * b + 1)
+            if b + 1 < BATCH:
+                x_bf16[b + 1] = channels_to_partitions(x_sb[b + 1], per_batch, "x_bf16")
             head_round(HEADS * b + 2)
             v_mx[b] = quantise(v_bf16[b][:].rearrange("p h c j -> p (h c j)"), per_batch, "v")
             head_round(HEADS * b + 3)
             if b + 1 < BATCH:
-                x_bf16[b + 1] = channels_to_partitions(x_sb[b + 1], per_batch, "x_bf16")
+                start_projection(b + 1)
         quantise_attn(ROUNDS - 1)
         for r in range(ROUNDS - OUTPUT_LAG, ROUNDS):
             output(r)

@@ -35,8 +35,8 @@ def tile_multiscaleretention_pa_t_kernel(tc, q, k, x, W_v, out):
         per_batch = ctx.enter_context(tc.tile_pool(name="per_batch", bufs=2))
         per_round = ctx.enter_context(tc.tile_pool(name="per_round", bufs=3))
         waiting = ctx.enter_context(tc.tile_pool(name="waiting", bufs=OUTPUT_LAG + 1))
-        psum_copy = ctx.enter_context(tc.psum_pool(name="psum_copy", bufs=4))
-        psum_s = ctx.enter_context(tc.psum_pool(name="psum_s", bufs=BLOCKS))
+        psum_copy = ctx.enter_context(tc.psum_pool(name="psum_copy", bufs=5))
+        psum_s = ctx.enter_context(tc.psum_pool(name="psum_s", bufs=BLOCKS - 1))
         ctx.enter_context(tc.manual_schedule())
 
         def load_rows(pool, matrix, name):
@@ -44,15 +44,17 @@ def tile_multiscaleretention_pa_t_kernel(tc, q, k, x, W_v, out):
             nc.sync.dma_start(out=rows[:], in_=matrix.rearrange("(r p) c -> p r c", p=P))
             return rows
 
-        k_sb, q_sb, x_sb = [], [], []
-        k_sb.append(load_rows(inputs, k[0], "k_sb"))
-        q_sb.append(load_rows(inputs, q[0], "q_sb"))
+        k_sb, q_sb, x_sb = {}, {}, {}
+
+        def load_batch(b):
+            if b < BATCH:
+                k_sb[b] = load_rows(inputs, k[b], "k_sb")
+                q_sb[b] = load_rows(inputs, q[b], "q_sb")
+                x_sb[b] = load_rows(inputs, x[b], "x_sb")
+
+        load_batch(0)
         w_sb = load_rows(const, W_v, "w_sb")
-        x_sb.append(load_rows(inputs, x[0], "x_sb"))
-        for b in range(1, BATCH):
-            k_sb.append(load_rows(inputs, k[b], "k_sb"))
-            q_sb.append(load_rows(inputs, q[b], "q_sb"))
-            x_sb.append(load_rows(inputs, x[b], "x_sb"))
+        load_batch(1)
 
         far_to_near = dict(pattern=[[1, P], [-P, BLOCKS]], base=P * (BLOCKS - 1), channel_multiplier=-1)
         distance = const.tile([P, P, BLOCKS], F32, name="distance")
@@ -121,7 +123,7 @@ def tile_multiscaleretention_pa_t_kernel(tc, q, k, x, W_v, out):
                     )
                 nc.scalar.copy(out=v_bf16[b][:, h, :, :], in_=v_ps[:].rearrange("p j c -> p c j"))
 
-        kq, s_ps, a_mx = {}, {}, {}
+        kq, s_ps, s0_sb, a_mx = {}, {}, {}, {}
 
         def head_channels_to_partitions(r):
             if r >= ROUNDS:
@@ -138,7 +140,10 @@ def tile_multiscaleretention_pa_t_kernel(tc, q, k, x, W_v, out):
         def scores(r, i):
             if r >= ROUNDS:
                 return
-            s_ps[i] = psum_s.tile([P, BLOCKS, P], F32, name="s_ps")
+            if i == 0:
+                s_ps[i] = psum_copy.tile([P, BLOCKS, P], F32, name="s0_ps", tag="copy")
+            else:
+                s_ps[i] = psum_s.tile([P, BLOCKS, P], F32, name="s_ps")
             for j in range(i + 1):
                 nc.tensor.matmul(
                     out=s_ps[i][:, j, :],
@@ -155,6 +160,20 @@ def tile_multiscaleretention_pa_t_kernel(tc, q, k, x, W_v, out):
                 in1=decay[r % HEADS][:, :, BLOCKS - 1 - i : BLOCKS],
                 op=mybir.AluOpType.mult,
             )
+
+        def first_block_out(r):
+            if r < ROUNDS:
+                s0_sb[r] = per_round.tile([P, P], F32, name="s0_sb")
+                nc.scalar.copy(out=s0_sb[r][:], in_=s_ps[0][:, 0, :])
+
+        def first_block_decay(r):
+            if r < ROUNDS:
+                nc.gpsimd.tensor_tensor(
+                    out=attn_bf16[r % 2][:, block(0), 0],
+                    in0=s0_sb[r][:],
+                    in1=decay[r % HEADS][:, :, BLOCKS - 1],
+                    op=mybir.AluOpType.mult,
+                )
 
         def quantise_attn(r):
             if r >= 0:
@@ -177,20 +196,21 @@ def tile_multiscaleretention_pa_t_kernel(tc, q, k, x, W_v, out):
                 )
             y_sb = per_round.tile([P, BLOCKS, P], F32, name="y_sb")
             nc.scalar.copy(out=y_sb[:], in_=y_ps[:])
-            nc.scalar.dma_start(
+            nc.sync.dma_start(
                 out=out[b][:, block(h)].rearrange("(i p) c -> p i c", p=P), in_=y_sb[:]
             )
 
         def head_round(r):
-            apply_decay(r, 0)
             scores(r + 1, 0)
-            quantise_attn(r - 1)
-            output(r - OUTPUT_LAG)
+            first_block_out(r + 1)
             apply_decay(r, 1)
             scores(r + 1, 1)
+            quantise_attn(r - 1)
+            first_block_decay(r + 1)
             head_channels_to_partitions(r + 2)
             apply_decay(r, 2)
             scores(r + 1, 2)
+            output(r - OUTPUT_LAG)
             apply_decay(r, 3)
             scores(r + 1, 3)
 
@@ -198,8 +218,10 @@ def tile_multiscaleretention_pa_t_kernel(tc, q, k, x, W_v, out):
         head_channels_to_partitions(1)
         for i in range(BLOCKS):
             scores(0, i)
-        w_bf16 = channels_to_partitions(w_sb, const, "w_bf16")
+        first_block_out(0)
+        first_block_decay(0)
         x_bf16[0] = channels_to_partitions(x_sb[0], per_batch, "x_bf16")
+        w_bf16 = channels_to_partitions(w_sb, const, "w_bf16")
 
         def start_projection(b):
             x_mx[b] = quantise(x_bf16[b][:], per_batch, "x")
@@ -208,6 +230,7 @@ def tile_multiscaleretention_pa_t_kernel(tc, q, k, x, W_v, out):
 
         for b in range(BATCH):
             head_round(HEADS * b)
+            load_batch(b + 2)
             if b == 0:
                 w_mx = quantise(w_bf16[:], const, "w")
                 start_projection(0)

@@ -19,6 +19,7 @@ HEADS = CHANNELS // P
 BLOCKS = TOKENS // P
 ROUNDS = BATCH * HEADS
 OUTPUT_LAG = 3
+TRANSPOSE_LEAD = 3
 
 FLOPS = 3 * 2 * BATCH * TOKENS * TOKENS * CHANNELS
 
@@ -34,6 +35,7 @@ def tile_multiscaleretention_pa_t_kernel(tc, q, k, x, W_v, out):
         inputs = ctx.enter_context(tc.tile_pool(name="inputs", bufs=BATCH))
         per_batch = ctx.enter_context(tc.tile_pool(name="per_batch", bufs=2))
         per_round = ctx.enter_context(tc.tile_pool(name="per_round", bufs=3))
+        transposed = ctx.enter_context(tc.tile_pool(name="transposed", bufs=TRANSPOSE_LEAD + 1))
         waiting = ctx.enter_context(tc.tile_pool(name="waiting", bufs=OUTPUT_LAG + 1))
         psum_copy = ctx.enter_context(tc.psum_pool(name="psum_copy", bufs=5))
         psum_s = ctx.enter_context(tc.psum_pool(name="psum_s", bufs=BLOCKS - 1))
@@ -134,16 +136,13 @@ def tile_multiscaleretention_pa_t_kernel(tc, q, k, x, W_v, out):
                 nc.tensor.transpose(kq_ps[:, 0, block(n)], k_sb[b][:, n, block(h)], ident_bf16[:])
             for n in range(BLOCKS):
                 nc.tensor.transpose(kq_ps[:, 1, block(n)], q_sb[b][:, n, block(h)], ident_bf16[:])
-            kq[r] = per_round.tile([P, 2, TOKENS], BF16, name="kq")
+            kq[r] = transposed.tile([P, 2, TOKENS], BF16, name="kq")
             nc.scalar.copy(out=kq[r][:], in_=kq_ps[:])
 
         def scores(r, i):
             if r >= ROUNDS:
                 return
-            if i == 0:
-                s_ps[i] = psum_copy.tile([P, BLOCKS, P], F32, name="s0_ps", tag="copy")
-            else:
-                s_ps[i] = psum_s.tile([P, BLOCKS, P], F32, name="s_ps")
+            s_ps[i] = psum_s.tile([P, BLOCKS, P], F32, name="s_ps")
             for j in range(i + 1):
                 nc.tensor.matmul(
                     out=s_ps[i][:, j, :],
@@ -161,16 +160,26 @@ def tile_multiscaleretention_pa_t_kernel(tc, q, k, x, W_v, out):
                 op=mybir.AluOpType.mult,
             )
 
-        def first_block_out(r):
-            if r < ROUNDS:
-                s0_sb[r] = per_round.tile([P, P], F32, name="s0_sb")
-                nc.scalar.copy(out=s0_sb[r][:], in_=s_ps[0][:, 0, :])
+        def first_block_scores(r):
+            if r >= ROUNDS:
+                return
+            s0_ps = psum_copy.tile([P, 2, P], F32, name="s0_ps", tag="copy")
+            for n in range(2):
+                nc.tensor.matmul(
+                    out=s0_ps[:, n, :],
+                    lhsT=kq[r + n][:, 0, block(0)],
+                    rhs=kq[r + n][:, 1, block(0)],
+                    start=True,
+                    stop=True,
+                )
+            s0_sb[r] = per_round.tile([P, 2, P], F32, name="s0_sb")
+            nc.scalar.copy(out=s0_sb[r][:], in_=s0_ps[:])
 
         def first_block_decay(r):
             if r < ROUNDS:
                 nc.gpsimd.tensor_tensor(
                     out=attn_bf16[r % 2][:, block(0), 0],
-                    in0=s0_sb[r][:],
+                    in0=s0_sb[r - r % 2][:, r % 2, :],
                     in1=decay[r % HEADS][:, :, BLOCKS - 1],
                     op=mybir.AluOpType.mult,
                 )
@@ -201,13 +210,13 @@ def tile_multiscaleretention_pa_t_kernel(tc, q, k, x, W_v, out):
             )
 
         def head_round(r):
-            scores(r + 1, 0)
-            first_block_out(r + 1)
+            if r % 2 == 1:
+                first_block_scores(r + 1)
             apply_decay(r, 1)
             scores(r + 1, 1)
             quantise_attn(r - 1)
             first_block_decay(r + 1)
-            head_channels_to_partitions(r + 2)
+            head_channels_to_partitions(r + TRANSPOSE_LEAD)
             apply_decay(r, 2)
             scores(r + 1, 2)
             output(r - OUTPUT_LAG)
@@ -216,9 +225,11 @@ def tile_multiscaleretention_pa_t_kernel(tc, q, k, x, W_v, out):
 
         head_channels_to_partitions(0)
         head_channels_to_partitions(1)
-        for i in range(BLOCKS):
+        for i in range(1, BLOCKS):
             scores(0, i)
-        first_block_out(0)
+        for r in range(2, TRANSPOSE_LEAD):
+            head_channels_to_partitions(r)
+        first_block_scores(0)
         first_block_decay(0)
         x_bf16[0] = channels_to_partitions(x_sb[0], per_batch, "x_bf16")
         w_bf16 = channels_to_partitions(w_sb, const, "w_bf16")

@@ -19,6 +19,7 @@ HEADS = CHANNELS // P
 BLOCKS = TOKENS // P
 ROUNDS = BATCH * HEADS
 OUTPUT_LAG = 3
+FAR = 2.0**20
 TRANSPOSE_LEAD = 3
 
 FLOPS = 3 * 2 * BATCH * TOKENS * TOKENS * CHANNELS
@@ -38,7 +39,7 @@ def tile_multiscaleretention_pa_t_kernel(tc, q, k, x, W_v, out):
         transposed = ctx.enter_context(tc.tile_pool(name="transposed", bufs=TRANSPOSE_LEAD + 1))
         waiting = ctx.enter_context(tc.tile_pool(name="waiting", bufs=OUTPUT_LAG + 1))
         psum_copy = ctx.enter_context(tc.psum_pool(name="psum_copy", bufs=5))
-        psum_s = ctx.enter_context(tc.psum_pool(name="psum_s", bufs=BLOCKS - 1))
+        psum_s = ctx.enter_context(tc.psum_pool(name="psum_s", bufs=3))
         ctx.enter_context(tc.manual_schedule())
 
         def load_rows(pool, matrix, name):
@@ -61,6 +62,15 @@ def tile_multiscaleretention_pa_t_kernel(tc, q, k, x, W_v, out):
         far_to_near = dict(pattern=[[1, P], [-P, BLOCKS]], base=P * (BLOCKS - 1), channel_multiplier=-1)
         distance = const.tile([P, P, BLOCKS], F32, name="distance")
         nc.gpsimd.iota(distance[:], allow_small_or_imprecise_dtypes=True, **far_to_near)
+        nc.gpsimd.affine_select(
+            out=distance[:, :, BLOCKS - 1],
+            in_=distance[:, :, BLOCKS - 1],
+            compare_op=mybir.AluOpType.is_ge,
+            fill=FAR,
+            pattern=[[1, P]],
+            base=0,
+            channel_multiplier=-1,
+        )
         ident_bf16 = const.tile([P, P], BF16, name="ident_bf16")
         make_identity(nc, ident_bf16[:])
         ident_f32 = const.tile([P, P], F32, name="ident_f32")
@@ -75,9 +85,6 @@ def tile_multiscaleretention_pa_t_kernel(tc, q, k, x, W_v, out):
                 func=mybir.ActivationFunctionType.Exp,
                 scale=math.log(1.0 - 2.0 ** (-5 - h)),
                 bias=-0.5 * math.log(P),
-            )
-            nc.gpsimd.affine_select(
-                out=table[:], in_=table[:], compare_op=mybir.AluOpType.is_ge, fill=0.0, **far_to_near
             )
             decay.append(table)
 
@@ -125,7 +132,7 @@ def tile_multiscaleretention_pa_t_kernel(tc, q, k, x, W_v, out):
                     )
                 nc.scalar.copy(out=v_bf16[b][:, h, :, :], in_=v_ps[:].rearrange("p j c -> p c j"))
 
-        kq, s_ps, s0_sb, a_mx = {}, {}, {}, {}
+        kq, s_ps, s01_sb, a_mx = {}, {}, {}, {}
 
         def head_channels_to_partitions(r):
             if r >= ROUNDS:
@@ -142,10 +149,10 @@ def tile_multiscaleretention_pa_t_kernel(tc, q, k, x, W_v, out):
         def scores(r, i):
             if r >= ROUNDS:
                 return
-            s_ps[i] = psum_s.tile([P, BLOCKS, P], F32, name="s_ps")
+            s_ps[r, i] = psum_s.tile([P, BLOCKS, P], F32, name="s_ps")
             for j in range(i + 1):
                 nc.tensor.matmul(
-                    out=s_ps[i][:, j, :],
+                    out=s_ps[r, i][:, j, :],
                     lhsT=kq[r][:, 0, block(j)],
                     rhs=kq[r][:, 1, block(i)],
                     start=True,
@@ -155,7 +162,7 @@ def tile_multiscaleretention_pa_t_kernel(tc, q, k, x, W_v, out):
         def apply_decay(r, i):
             nc.vector.tensor_tensor(
                 out=attn_bf16[r % 2][:, block(i), 0 : i + 1],
-                in0=s_ps[i][:, 0 : i + 1, :].rearrange("p j t -> p t j"),
+                in0=s_ps[r, i][:, 0 : i + 1, :].rearrange("p j t -> p t j"),
                 in1=decay[r % HEADS][:, :, BLOCKS - 1 - i : BLOCKS],
                 op=mybir.AluOpType.mult,
             )
@@ -163,26 +170,33 @@ def tile_multiscaleretention_pa_t_kernel(tc, q, k, x, W_v, out):
         def first_block_scores(r):
             if r >= ROUNDS:
                 return
-            s0_ps = psum_copy.tile([P, 2, P], F32, name="s0_ps", tag="copy")
-            for n in range(2):
+            s01_ps = psum_copy.tile([P, 3, P], F32, name="s01_ps", tag="copy")
+            for place, (i, j) in enumerate(((0, 0), (1, 0), (1, 1))):
                 nc.tensor.matmul(
-                    out=s0_ps[:, n, :],
-                    lhsT=kq[r + n][:, 0, block(0)],
-                    rhs=kq[r + n][:, 1, block(0)],
+                    out=s01_ps[:, place, :],
+                    lhsT=kq[r][:, 0, block(j)],
+                    rhs=kq[r][:, 1, block(i)],
                     start=True,
                     stop=True,
                 )
-            s0_sb[r] = per_round.tile([P, 2, P], F32, name="s0_sb")
-            nc.scalar.copy(out=s0_sb[r][:], in_=s0_ps[:])
+            s01_sb[r] = per_round.tile([P, 3, P], F32, name="s01_sb")
+            nc.scalar.copy(out=s01_sb[r][:], in_=s01_ps[:])
 
         def first_block_decay(r):
-            if r < ROUNDS:
-                nc.gpsimd.tensor_tensor(
-                    out=attn_bf16[r % 2][:, block(0), 0],
-                    in0=s0_sb[r - r % 2][:, r % 2, :],
-                    in1=decay[r % HEADS][:, :, BLOCKS - 1],
-                    op=mybir.AluOpType.mult,
-                )
+            if r >= ROUNDS:
+                return
+            nc.gpsimd.tensor_tensor(
+                out=attn_bf16[r % 2][:, block(0), 0],
+                in0=s01_sb[r][:, 0, :],
+                in1=decay[r % HEADS][:, :, BLOCKS - 1],
+                op=mybir.AluOpType.mult,
+            )
+            nc.gpsimd.tensor_tensor(
+                out=attn_bf16[r % 2][:, block(1), 0:2],
+                in0=s01_sb[r][:, 1:3, :].rearrange("p j t -> p t j"),
+                in1=decay[r % HEADS][:, :, BLOCKS - 2 : BLOCKS],
+                op=mybir.AluOpType.mult,
+            )
 
         def quantise_attn(r):
             if r >= 0:
@@ -209,51 +223,59 @@ def tile_multiscaleretention_pa_t_kernel(tc, q, k, x, W_v, out):
                 out=out[b][:, block(h)].rearrange("(i p) c -> p i c", p=P), in_=y_sb[:]
             )
 
-        def head_round(r):
-            if r % 2 == 1:
-                first_block_scores(r + 1)
-            apply_decay(r, 1)
-            scores(r + 1, 1)
-            quantise_attn(r - 1)
-            first_block_decay(r + 1)
-            head_channels_to_partitions(r + TRANSPOSE_LEAD)
-            apply_decay(r, 2)
+        def head_round(r, value_path=()):
             scores(r + 1, 2)
-            output(r - OUTPUT_LAG)
+            first_block_scores(r + 2)
+            apply_decay(r, 2)
+            head_channels_to_partitions(r + TRANSPOSE_LEAD)
             apply_decay(r, 3)
             scores(r + 1, 3)
+            output(r - OUTPUT_LAG)
+            for step in value_path:
+                step()
+            quantise_attn(r - 1)
+            first_block_decay(r + 1)
 
         head_channels_to_partitions(0)
         head_channels_to_partitions(1)
-        for i in range(1, BLOCKS):
-            scores(0, i)
+        scores(0, 2)
+        scores(0, 3)
+        first_block_scores(0)
+        first_block_scores(1)
+        first_block_decay(0)
         for r in range(2, TRANSPOSE_LEAD):
             head_channels_to_partitions(r)
-        first_block_scores(0)
-        first_block_decay(0)
         x_bf16[0] = channels_to_partitions(x_sb[0], per_batch, "x_bf16")
         w_bf16 = channels_to_partitions(w_sb, const, "w_bf16")
+        w_mx = []
 
         def start_projection(b):
             x_mx[b] = quantise(x_bf16[b][:], per_batch, "x")
             v_bf16[b] = per_batch.tile([P, HEADS, P, PACK], BF16, name="v_bf16", align_bytes=64)
             project_values(b, (0, 1))
 
-        for b in range(BATCH):
-            head_round(HEADS * b)
+        def first_value_path():
+            load_batch(2)
+            w_mx.extend(quantise(w_bf16[:], const, "w"))
+            start_projection(0)
+            project_values(0, (2, 3))
+
+        def finish_projection(b):
             load_batch(b + 2)
-            if b == 0:
-                w_mx = quantise(w_bf16[:], const, "w")
-                start_projection(0)
             project_values(b, (2, 3))
-            head_round(HEADS * b + 1)
-            if b + 1 < BATCH:
-                x_bf16[b + 1] = channels_to_partitions(x_sb[b + 1], per_batch, "x_bf16")
-            head_round(HEADS * b + 2)
+
+        def transpose_x(b):
+            x_bf16[b] = channels_to_partitions(x_sb[b], per_batch, "x_bf16")
+
+        def quantise_values(b):
             v_mx[b] = quantise(v_bf16[b][:].rearrange("p h c j -> p (h c j)"), per_batch, "v")
-            head_round(HEADS * b + 3)
-            if b + 1 < BATCH:
-                start_projection(b + 1)
+
+        for b in range(BATCH):
+            last = b + 1 == BATCH
+            head_round(HEADS * b, [first_value_path if b == 0 else lambda: finish_projection(b)])
+            head_round(HEADS * b + 1, [] if last else [lambda: transpose_x(b + 1)])
+            head_round(HEADS * b + 2, [lambda: quantise_values(b)])
+            head_round(HEADS * b + 3, [] if last else [lambda: start_projection(b + 1)])
         quantise_attn(ROUNDS - 1)
         for r in range(ROUNDS - OUTPUT_LAG, ROUNDS):
             output(r)

@@ -18,9 +18,11 @@ CHANNELS = 512
 HEADS = CHANNELS // P
 BLOCKS = TOKENS // P
 ROUNDS = BATCH * HEADS
-OUTPUT_LAG = 3
+OUTPUT_LAG = 2
+TRANSPOSE_LEAD = 2
+LOAD_LEAD = 3
+X_LEAD = BLOCKS + 2
 FAR = 2.0**20
-TRANSPOSE_LEAD = 3
 
 FLOPS = 3 * 2 * BATCH * TOKENS * TOKENS * CHANNELS
 
@@ -38,8 +40,8 @@ def tile_multiscaleretention_pa_t_kernel(tc, q, k, x, W_v, out):
         per_round = ctx.enter_context(tc.tile_pool(name="per_round", bufs=3))
         transposed = ctx.enter_context(tc.tile_pool(name="transposed", bufs=TRANSPOSE_LEAD + 1))
         waiting = ctx.enter_context(tc.tile_pool(name="waiting", bufs=OUTPUT_LAG + 1))
-        psum_copy = ctx.enter_context(tc.psum_pool(name="psum_copy", bufs=5))
-        psum_s = ctx.enter_context(tc.psum_pool(name="psum_s", bufs=3))
+        psum_scalar = ctx.enter_context(tc.psum_pool(name="psum_scalar", bufs=4))
+        psum_vector = ctx.enter_context(tc.psum_pool(name="psum_vector", bufs=4))
         ctx.enter_context(tc.manual_schedule())
 
         def load_rows(pool, matrix, name):
@@ -57,11 +59,17 @@ def tile_multiscaleretention_pa_t_kernel(tc, q, k, x, W_v, out):
 
         load_batch(0)
         w_sb = load_rows(const, W_v, "w_sb")
-        load_batch(1)
+        for b in range(1, LOAD_LEAD):
+            load_batch(b)
 
-        far_to_near = dict(pattern=[[1, P], [-P, BLOCKS]], base=P * (BLOCKS - 1), channel_multiplier=-1)
         distance = const.tile([P, P, BLOCKS], F32, name="distance")
-        nc.gpsimd.iota(distance[:], allow_small_or_imprecise_dtypes=True, **far_to_near)
+        nc.gpsimd.iota(
+            distance[:],
+            pattern=[[1, P], [-P, BLOCKS]],
+            base=P * (BLOCKS - 1),
+            channel_multiplier=-1,
+            allow_small_or_imprecise_dtypes=True,
+        )
         nc.gpsimd.affine_select(
             out=distance[:, :, BLOCKS - 1],
             in_=distance[:, :, BLOCKS - 1],
@@ -76,8 +84,15 @@ def tile_multiscaleretention_pa_t_kernel(tc, q, k, x, W_v, out):
         ident_f32 = const.tile([P, P], F32, name="ident_f32")
         make_identity(nc, ident_f32[:])
 
+        attn_bf16 = []
+        for n in range(2):
+            zeroed = const.tile([P, TOKENS, PACK], BF16, name="attn_bf16_%d" % n, align_bytes=64)
+            nc.vector.memset(zeroed[:], 0.0)
+            attn_bf16.append(zeroed)
+
         decay = []
-        for h in range(HEADS):
+
+        def make_decay(h):
             table = const.tile([P, P, BLOCKS], F32, name="decay_%d" % h)
             nc.scalar.activation(
                 out=table[:],
@@ -88,49 +103,53 @@ def tile_multiscaleretention_pa_t_kernel(tc, q, k, x, W_v, out):
             )
             decay.append(table)
 
-        attn_bf16 = []
-        for n in range(2):
-            zeroed = const.tile([P, TOKENS, PACK], BF16, name="attn_bf16_%d" % n, align_bytes=64)
-            nc.vector.memset(zeroed[:], 0.0)
-            attn_bf16.append(zeroed)
-
-        def channels_to_partitions(rows, pool, name):
-            grouped = pool.tile([P, TOKENS * PACK], BF16, name=name, align_bytes=64)
-            pairs = grouped[:].bitcast(F32).rearrange("p (n u) -> p n u", u=2)
-            for half in range(2):
-                bank = psum_copy.tile([P, 2, 2 * P], F32, name="pairs_ps", tag="copy")
-                for r in range(2):
-                    row_pairs = rows[:, 2 * half + r, :].bitcast(F32)
-                    for u in range(2):
-                        nc.tensor.transpose(bank[:, u, block(r)], row_pairs[:, block(u)], ident_f32[:])
-                nc.scalar.copy(
-                    out=pairs[:, 2 * P * half : 2 * P * (half + 1), :],
-                    in_=bank[:].rearrange("p u n -> p n u"),
-                )
-            return grouped
-
         def quantise(grouped, pool, name):
-            words = pool.tile([P, TOKENS], U32, name=name + "_words", align_bytes=64)
-            scales = pool.tile([P, TOKENS], U8, name=name + "_scales", align_bytes=64)
+            n = grouped.shape[1] // PACK
+            words = pool.tile([P, n], U32, name=name + "_words", align_bytes=64)
+            scales = pool.tile([P, n], U8, name=name + "_scales", align_bytes=64)
             nc.vector.quantize_mx(out=words[:].bitcast(FP8X4), scales=scales[:], in_=grouped)
             return words, scales
 
-        x_bf16, x_mx, v_bf16, v_mx = {}, {}, {}, {}
+        def new_grouped(pool, name):
+            return pool.tile([P, TOKENS * PACK], BF16, name=name, align_bytes=64)
 
-        def project_values(b, heads):
-            for h in heads:
-                v_ps = psum_copy.tile([P, BLOCKS, P], F32, name="v_ps", tag="copy")
-                for j in range(BLOCKS):
-                    nc.tensor.matmul_mx(
-                        out=v_ps[:, j, :],
-                        lhsT=x_mx[b][0][:, block(j)].bitcast(FP8X4),
-                        lhsT_scale=x_mx[b][1][:, block(j)],
-                        rhs=w_mx[0][:, block(h)].bitcast(FP8X4),
-                        rhs_scale=w_mx[1][:, block(h)],
-                        start=True,
-                        stop=True,
-                    )
-                nc.scalar.copy(out=v_bf16[b][:, h, :, :], in_=v_ps[:].rearrange("p j c -> p c j"))
+        def transpose_pairs(rows, places, psum):
+            bank = psum.tile([P, 2, len(places) * P], F32, name="pairs_ps", tag="bank")
+            for n, r in enumerate(places):
+                row_pairs = rows[:, r, :].bitcast(F32)
+                for u in range(2):
+                    nc.tensor.transpose(bank[:, u, block(n)], row_pairs[:, block(u)], ident_f32[:])
+            return bank
+
+        def copy_pairs(copy, bank, grouped, places):
+            pairs = grouped[:].bitcast(F32).rearrange("p (n u) -> p n u", u=2)
+            copy(
+                out=pairs[:, P * places[0] : P * (places[-1] + 1), :],
+                in_=bank[:].rearrange("p u n -> p n u"),
+            )
+
+        x_bf16, x_mx, v_mx = {}, {}, {}
+
+        def project_values(r):
+            b, h = divmod(r, HEADS)
+            v_ps = psum_scalar.tile([P, BLOCKS, P], F32, name="v_ps", tag="bank")
+            for j in range(BLOCKS):
+                nc.tensor.matmul_mx(
+                    out=v_ps[:, j, :],
+                    lhsT=x_mx[b][0][:, block(j)].bitcast(FP8X4),
+                    lhsT_scale=x_mx[b][1][:, block(j)],
+                    rhs=w_mx[0][:, block(h)].bitcast(FP8X4),
+                    rhs_scale=w_mx[1][:, block(h)],
+                    start=True,
+                    stop=True,
+                )
+            v_bf16 = per_round.tile([P, P, PACK], BF16, name="v_bf16", align_bytes=64)
+            nc.scalar.copy(out=v_bf16[:], in_=v_ps[:].rearrange("p j c -> p c j"))
+            v_mx[r] = v_bf16
+
+        def quantise_values(r):
+            if r >= 0:
+                v_mx[r] = quantise(v_mx[r][:].rearrange("p c j -> p (c j)"), waiting, "v")
 
         kq, s_ps, s01_sb, a_mx = {}, {}, {}, {}
 
@@ -138,26 +157,28 @@ def tile_multiscaleretention_pa_t_kernel(tc, q, k, x, W_v, out):
             if r >= ROUNDS:
                 return
             b, h = divmod(r, HEADS)
-            kq_ps = psum_copy.tile([P, 2, TOKENS], BF16, name="kq_ps", tag="copy")
-            for n in range(BLOCKS):
-                nc.tensor.transpose(kq_ps[:, 0, block(n)], k_sb[b][:, n, block(h)], ident_bf16[:])
-            for n in range(BLOCKS):
-                nc.tensor.transpose(kq_ps[:, 1, block(n)], q_sb[b][:, n, block(h)], ident_bf16[:])
+            kq_ps = psum_scalar.tile([P, 2, TOKENS], BF16, name="kq_ps", tag="bank")
+            for side, rows in enumerate((k_sb[b], q_sb[b])):
+                for n in range(BLOCKS):
+                    nc.tensor.transpose(kq_ps[:, side, block(n)], rows[:, n, block(h)], ident_bf16[:])
             kq[r] = transposed.tile([P, 2, TOKENS], BF16, name="kq")
             nc.scalar.copy(out=kq[r][:], in_=kq_ps[:])
 
-        def scores(r, i):
-            if r >= ROUNDS:
-                return
-            s_ps[r, i] = psum_s.tile([P, BLOCKS, P], F32, name="s_ps")
-            for j in range(i + 1):
+        def score_blocks(r, bank, places):
+            for n, (i, j) in enumerate(places):
                 nc.tensor.matmul(
-                    out=s_ps[r, i][:, j, :],
+                    out=bank[:, n, :],
                     lhsT=kq[r][:, 0, block(j)],
                     rhs=kq[r][:, 1, block(i)],
                     start=True,
                     stop=True,
                 )
+
+        def scores(r, i):
+            if r >= ROUNDS:
+                return
+            s_ps[r, i] = psum_vector.tile([P, BLOCKS, P], F32, name="s_ps", tag="bank")
+            score_blocks(r, s_ps[r, i], [(i, j) for j in range(i + 1)])
 
         def apply_decay(r, i):
             nc.vector.tensor_tensor(
@@ -170,21 +191,12 @@ def tile_multiscaleretention_pa_t_kernel(tc, q, k, x, W_v, out):
         def first_block_scores(r):
             if r >= ROUNDS:
                 return
-            s01_ps = psum_copy.tile([P, 3, P], F32, name="s01_ps", tag="copy")
-            for place, (i, j) in enumerate(((0, 0), (1, 0), (1, 1))):
-                nc.tensor.matmul(
-                    out=s01_ps[:, place, :],
-                    lhsT=kq[r][:, 0, block(j)],
-                    rhs=kq[r][:, 1, block(i)],
-                    start=True,
-                    stop=True,
-                )
+            s01_ps = psum_scalar.tile([P, 3, P], F32, name="s01_ps", tag="bank")
+            score_blocks(r, s01_ps, [(0, 0), (1, 0), (1, 1)])
             s01_sb[r] = per_round.tile([P, 3, P], F32, name="s01_sb")
             nc.scalar.copy(out=s01_sb[r][:], in_=s01_ps[:])
 
         def first_block_decay(r):
-            if r >= ROUNDS:
-                return
             nc.gpsimd.tensor_tensor(
                 out=attn_bf16[r % 2][:, block(0), 0],
                 in0=s01_sb[r][:, 0, :],
@@ -206,14 +218,14 @@ def tile_multiscaleretention_pa_t_kernel(tc, q, k, x, W_v, out):
             if r < 0:
                 return
             b, h = divmod(r, HEADS)
-            y_ps = psum_copy.tile([P, BLOCKS, P], F32, name="y_ps", tag="copy")
+            y_ps = psum_scalar.tile([P, BLOCKS, P], F32, name="y_ps", tag="bank")
             for i in range(BLOCKS):
                 nc.tensor.matmul_mx(
                     out=y_ps[:, i, :],
                     lhsT=a_mx[r][0][:, block(i)].bitcast(FP8X4),
                     lhsT_scale=a_mx[r][1][:, block(i)],
-                    rhs=v_mx[b][0][:, block(h)].bitcast(FP8X4),
-                    rhs_scale=v_mx[b][1][:, block(h)],
+                    rhs=v_mx[r][0][:].bitcast(FP8X4),
+                    rhs_scale=v_mx[r][1][:],
                     start=True,
                     stop=True,
                 )
@@ -223,59 +235,70 @@ def tile_multiscaleretention_pa_t_kernel(tc, q, k, x, W_v, out):
                 out=out[b][:, block(h)].rearrange("(i p) c -> p i c", p=P), in_=y_sb[:]
             )
 
-        def head_round(r, value_path=()):
-            scores(r + 1, 2)
-            first_block_scores(r + 2)
-            apply_decay(r, 2)
-            head_channels_to_partitions(r + TRANSPOSE_LEAD)
-            apply_decay(r, 3)
-            scores(r + 1, 3)
-            output(r - OUTPUT_LAG)
-            for step in value_path:
-                step()
-            quantise_attn(r - 1)
-            first_block_decay(r + 1)
+        def x_quarters(done, upto):
+            banks = []
+            for n in range(done, min(upto, BATCH * BLOCKS)):
+                b, place = divmod(n, BLOCKS)
+                if place == 0:
+                    x_bf16[b] = new_grouped(per_batch, "x_bf16")
+                banks.append((transpose_pairs(x_sb[b], [place], psum_vector), x_bf16[b], [place]))
+            return banks
 
+        def head_round(r):
+            b, h = divmod(r, HEADS)
+            if h == 0:
+                load_batch(b + LOAD_LEAD)
+            first_block_decay(r)
+            apply_decay(r, 2)
+            apply_decay(r, 3)
+            if r == 0:
+                copy_first_x()
+            scores(r + 1, 2)
+            first_block_scores(r + 1)
+            if r + 1 < HEADS:
+                make_decay(r + 1)
+            head_channels_to_partitions(r + TRANSPOSE_LEAD)
+            banks = x_quarters(BLOCKS if r == 0 else r + X_LEAD - 1, r + X_LEAD)
+            scores(r + 1, 3)
+            if r == 0:
+                first_values()
+            output(r - OUTPUT_LAG)
+            if h == HEADS - 1 and b + 1 < BATCH:
+                x_mx[b + 1] = quantise(x_bf16[b + 1][:], per_batch, "x")
+            for bank in banks:
+                copy_pairs(nc.vector.tensor_copy, *bank)
+            if r + 1 < ROUNDS:
+                project_values(r + 1)
+            quantise_values(r - 1)
+            quantise_attn(r - 1)
+
+        make_decay(0)
         head_channels_to_partitions(0)
         head_channels_to_partitions(1)
         scores(0, 2)
         scores(0, 3)
         first_block_scores(0)
-        first_block_scores(1)
-        first_block_decay(0)
-        for r in range(2, TRANSPOSE_LEAD):
-            head_channels_to_partitions(r)
-        x_bf16[0] = channels_to_partitions(x_sb[0], per_batch, "x_bf16")
-        w_bf16 = channels_to_partitions(w_sb, const, "w_bf16")
+        halves = ([0, 1], [2, 3])
+        x_banks = [transpose_pairs(x_sb[0], half, psum_vector) for half in halves]
+        w_banks = [transpose_pairs(w_sb, half, psum_scalar) for half in halves]
+        x_bf16[0] = new_grouped(per_batch, "x_bf16")
+        w_bf16 = new_grouped(const, "w_bf16")
+        for half, bank in zip(halves, w_banks):
+            copy_pairs(nc.scalar.copy, bank, w_bf16, half)
         w_mx = []
 
-        def start_projection(b):
-            x_mx[b] = quantise(x_bf16[b][:], per_batch, "x")
-            v_bf16[b] = per_batch.tile([P, HEADS, P, PACK], BF16, name="v_bf16", align_bytes=64)
-            project_values(b, (0, 1))
+        def copy_first_x():
+            for half, bank in zip(halves, x_banks):
+                copy_pairs(nc.vector.tensor_copy, bank, x_bf16[0], half)
 
-        def first_value_path():
-            load_batch(2)
+        def first_values():
+            x_mx[0] = quantise(x_bf16[0][:], per_batch, "x")
             w_mx.extend(quantise(w_bf16[:], const, "w"))
-            start_projection(0)
-            project_values(0, (2, 3))
+            project_values(0)
 
-        def finish_projection(b):
-            load_batch(b + 2)
-            project_values(b, (2, 3))
-
-        def transpose_x(b):
-            x_bf16[b] = channels_to_partitions(x_sb[b], per_batch, "x_bf16")
-
-        def quantise_values(b):
-            v_mx[b] = quantise(v_bf16[b][:].rearrange("p h c j -> p (h c j)"), per_batch, "v")
-
-        for b in range(BATCH):
-            last = b + 1 == BATCH
-            head_round(HEADS * b, [first_value_path if b == 0 else lambda: finish_projection(b)])
-            head_round(HEADS * b + 1, [] if last else [lambda: transpose_x(b + 1)])
-            head_round(HEADS * b + 2, [lambda: quantise_values(b)])
-            head_round(HEADS * b + 3, [] if last else [lambda: start_projection(b + 1)])
+        for r in range(ROUNDS):
+            head_round(r)
+        quantise_values(ROUNDS - 1)
         quantise_attn(ROUNDS - 1)
         for r in range(ROUNDS - OUTPUT_LAG, ROUNDS):
             output(r)

@@ -18,10 +18,9 @@ CHANNELS = 512
 HEADS = CHANNELS // P
 BLOCKS = TOKENS // P
 ROUNDS = BATCH * HEADS
-OUTPUT_LAG = 2
+OUTPUT_LAG = 3
 TRANSPOSE_LEAD = 2
 LOAD_LEAD = 3
-X_LEAD = BLOCKS + 2
 FAR = 2.0**20
 
 FLOPS = 3 * 2 * BATCH * TOKENS * TOKENS * CHANNELS
@@ -128,9 +127,11 @@ def tile_multiscaleretention_pa_t_kernel(tc, q, k, x, W_v, out):
                 in_=bank[:].rearrange("p u n -> p n u"),
             )
 
-        x_bf16, x_mx, v_mx = {}, {}, {}
+        x_bf16, x_mx, v_bf16, v_mx = {}, {}, {}, {}
 
         def project_values(r):
+            if r >= ROUNDS:
+                return
             b, h = divmod(r, HEADS)
             v_ps = psum_scalar.tile([P, BLOCKS, P], F32, name="v_ps", tag="bank")
             for j in range(BLOCKS):
@@ -143,15 +144,15 @@ def tile_multiscaleretention_pa_t_kernel(tc, q, k, x, W_v, out):
                     start=True,
                     stop=True,
                 )
-            v_bf16 = per_round.tile([P, P, PACK], BF16, name="v_bf16", align_bytes=64)
-            nc.scalar.copy(out=v_bf16[:], in_=v_ps[:].rearrange("p j c -> p c j"))
-            v_mx[r] = v_bf16
+            if r % 2 == 0:
+                v_bf16[r // 2] = per_round.tile([P, 2, P, PACK], BF16, name="v_bf16", align_bytes=64)
+            nc.scalar.copy(out=v_bf16[r // 2][:, r % 2], in_=v_ps[:].rearrange("p j c -> p c j"))
 
-        def quantise_values(r):
-            if r >= 0:
-                v_mx[r] = quantise(v_mx[r][:].rearrange("p c j -> p (c j)"), waiting, "v")
+        def quantise_values(pair):
+            grouped = v_bf16[pair][:].rearrange("p n c j -> p (n c j)")
+            v_mx[pair] = quantise(grouped, waiting, "v")
 
-        kq, s_ps, s01_sb, a_mx = {}, {}, {}, {}
+        kq, s_ps, s0_sb, a_mx = {}, {}, {}, {}
 
         def head_channels_to_partitions(r):
             if r >= ROUNDS:
@@ -191,22 +192,16 @@ def tile_multiscaleretention_pa_t_kernel(tc, q, k, x, W_v, out):
         def first_block_scores(r):
             if r >= ROUNDS:
                 return
-            s01_ps = psum_scalar.tile([P, 3, P], F32, name="s01_ps", tag="bank")
-            score_blocks(r, s01_ps, [(0, 0), (1, 0), (1, 1)])
-            s01_sb[r] = per_round.tile([P, 3, P], F32, name="s01_sb")
-            nc.scalar.copy(out=s01_sb[r][:], in_=s01_ps[:])
+            s0_ps = psum_scalar.tile([P, 1, P], F32, name="s0_ps", tag="bank")
+            score_blocks(r, s0_ps, [(0, 0)])
+            s0_sb[r] = per_round.tile([P, P], F32, name="s0_sb")
+            nc.scalar.copy(out=s0_sb[r][:], in_=s0_ps[:, 0, :])
 
         def first_block_decay(r):
             nc.gpsimd.tensor_tensor(
                 out=attn_bf16[r % 2][:, block(0), 0],
-                in0=s01_sb[r][:, 0, :],
+                in0=s0_sb[r][:],
                 in1=decay[r % HEADS][:, :, BLOCKS - 1],
-                op=mybir.AluOpType.mult,
-            )
-            nc.gpsimd.tensor_tensor(
-                out=attn_bf16[r % 2][:, block(1), 0:2],
-                in0=s01_sb[r][:, 1:3, :].rearrange("p j t -> p t j"),
-                in1=decay[r % HEADS][:, :, BLOCKS - 2 : BLOCKS],
                 op=mybir.AluOpType.mult,
             )
 
@@ -224,8 +219,8 @@ def tile_multiscaleretention_pa_t_kernel(tc, q, k, x, W_v, out):
                     out=y_ps[:, i, :],
                     lhsT=a_mx[r][0][:, block(i)].bitcast(FP8X4),
                     lhsT_scale=a_mx[r][1][:, block(i)],
-                    rhs=v_mx[r][0][:].bitcast(FP8X4),
-                    rhs_scale=v_mx[r][1][:],
+                    rhs=v_mx[r // 2][0][:, block(r % 2)].bitcast(FP8X4),
+                    rhs_scale=v_mx[r // 2][1][:, block(r % 2)],
                     start=True,
                     stop=True,
                 )
@@ -235,70 +230,66 @@ def tile_multiscaleretention_pa_t_kernel(tc, q, k, x, W_v, out):
                 out=out[b][:, block(h)].rearrange("(i p) c -> p i c", p=P), in_=y_sb[:]
             )
 
-        def x_quarters(done, upto):
-            banks = []
-            for n in range(done, min(upto, BATCH * BLOCKS)):
-                b, place = divmod(n, BLOCKS)
-                if place == 0:
-                    x_bf16[b] = new_grouped(per_batch, "x_bf16")
-                banks.append((transpose_pairs(x_sb[b], [place], psum_vector), x_bf16[b], [place]))
-            return banks
+        def transpose_x(n):
+            b, place = divmod(n, BLOCKS)
+            if place == 0:
+                x_bf16[b] = new_grouped(per_batch, "x_bf16")
+            copy_pairs(nc.scalar.copy, transpose_pairs(x_sb[b], [place], psum_scalar), x_bf16[b], [place])
+
+        x_quarters = [[r + 6] if r + 6 < BATCH * BLOCKS else [] for r in range(ROUNDS)]
+        x_quarters[0] = [4, 5]
+        x_quarters[1] = [6, 7]
 
         def head_round(r):
             b, h = divmod(r, HEADS)
             if h == 0:
                 load_batch(b + LOAD_LEAD)
             first_block_decay(r)
-            apply_decay(r, 2)
-            apply_decay(r, 3)
+            for i in range(1, BLOCKS):
+                apply_decay(r, i)
             if r == 0:
-                copy_first_x()
-            scores(r + 1, 2)
+                first_x_and_w()
+            scores(r + 1, 1)
             first_block_scores(r + 1)
-            if r + 1 < HEADS:
-                make_decay(r + 1)
             head_channels_to_partitions(r + TRANSPOSE_LEAD)
-            banks = x_quarters(BLOCKS if r == 0 else r + X_LEAD - 1, r + X_LEAD)
+            for n in x_quarters[r]:
+                transpose_x(n)
+            scores(r + 1, 2)
+            output(r - OUTPUT_LAG)
+            if h == 2 and b + 1 < BATCH:
+                x_mx[b + 1] = quantise(x_bf16[b + 1][:], per_batch, "x")
             scores(r + 1, 3)
             if r == 0:
-                first_values()
-            output(r - OUTPUT_LAG)
-            if h == HEADS - 1 and b + 1 < BATCH:
-                x_mx[b + 1] = quantise(x_bf16[b + 1][:], per_batch, "x")
-            for bank in banks:
-                copy_pairs(nc.vector.tensor_copy, *bank)
-            if r + 1 < ROUNDS:
-                project_values(r + 1)
-            quantise_values(r - 1)
+                project_values(0)
+            project_values(r + 1)
+            if r % 2 == 0 and r > 0:
+                quantise_values(r // 2 - 1)
             quantise_attn(r - 1)
 
-        make_decay(0)
+        for h in range(HEADS):
+            make_decay(h)
         head_channels_to_partitions(0)
         head_channels_to_partitions(1)
-        scores(0, 2)
-        scores(0, 3)
+        for i in range(1, BLOCKS):
+            scores(0, i)
         first_block_scores(0)
-        halves = ([0, 1], [2, 3])
-        x_banks = [transpose_pairs(x_sb[0], half, psum_vector) for half in halves]
-        w_banks = [transpose_pairs(w_sb, half, psum_scalar) for half in halves]
-        x_bf16[0] = new_grouped(per_batch, "x_bf16")
         w_bf16 = new_grouped(const, "w_bf16")
-        for half, bank in zip(halves, w_banks):
-            copy_pairs(nc.scalar.copy, bank, w_bf16, half)
+        x_bf16[0] = new_grouped(per_batch, "x_bf16")
         w_mx = []
 
-        def copy_first_x():
-            for half, bank in zip(halves, x_banks):
+        def first_x_and_w():
+            halves = ([0, 1], [2, 3])
+            for half in halves:
+                bank = transpose_pairs(x_sb[0], half, psum_vector)
                 copy_pairs(nc.vector.tensor_copy, bank, x_bf16[0], half)
-
-        def first_values():
+            for half in halves:
+                copy_pairs(nc.scalar.copy, transpose_pairs(w_sb, half, psum_scalar), w_bf16, half)
             x_mx[0] = quantise(x_bf16[0][:], per_batch, "x")
             w_mx.extend(quantise(w_bf16[:], const, "w"))
-            project_values(0)
 
         for r in range(ROUNDS):
             head_round(r)
-        quantise_values(ROUNDS - 1)
+        quantise_values(ROUNDS // 2 - 1)
         quantise_attn(ROUNDS - 1)
         for r in range(ROUNDS - OUTPUT_LAG, ROUNDS):
             output(r)

@@ -21,6 +21,8 @@ ROUNDS = BATCH * HEADS
 OUTPUT_LAG = 3
 TRANSPOSE_LEAD = 2
 LOAD_LEAD = 3
+X_ROUND = 1
+HALVES = ([0, 1], [2, 3])
 FAR = 2.0**20
 
 FLOPS = 3 * 2 * BATCH * TOKENS * TOKENS * CHANNELS
@@ -230,15 +232,11 @@ def tile_multiscaleretention_pa_t_kernel(tc, q, k, x, W_v, out):
                 out=out[b][:, block(h)].rearrange("(i p) c -> p i c", p=P), in_=y_sb[:]
             )
 
-        def transpose_x(n):
-            b, place = divmod(n, BLOCKS)
-            if place == 0:
-                x_bf16[b] = new_grouped(per_batch, "x_bf16")
-            copy_pairs(nc.scalar.copy, transpose_pairs(x_sb[b], [place], psum_scalar), x_bf16[b], [place])
-
-        x_quarters = [[r + 6] if r + 6 < BATCH * BLOCKS else [] for r in range(ROUNDS)]
-        x_quarters[0] = [4, 5]
-        x_quarters[1] = [6, 7]
+        def transpose_x(b):
+            x_bf16[b] = new_grouped(per_batch, "x_bf16")
+            banks = [transpose_pairs(x_sb[b], half, psum_scalar) for half in HALVES]
+            for half, bank in zip(HALVES, banks):
+                copy_pairs(nc.scalar.copy, bank, x_bf16[b], half)
 
         def head_round(r):
             b, h = divmod(r, HEADS)
@@ -252,8 +250,8 @@ def tile_multiscaleretention_pa_t_kernel(tc, q, k, x, W_v, out):
             scores(r + 1, 1)
             first_block_scores(r + 1)
             head_channels_to_partitions(r + TRANSPOSE_LEAD)
-            for n in x_quarters[r]:
-                transpose_x(n)
+            if h == X_ROUND and b + 1 < BATCH:
+                transpose_x(b + 1)
             scores(r + 1, 2)
             output(r - OUTPUT_LAG)
             if h == 2 and b + 1 < BATCH:
@@ -278,11 +276,10 @@ def tile_multiscaleretention_pa_t_kernel(tc, q, k, x, W_v, out):
         w_mx = []
 
         def first_x_and_w():
-            halves = ([0, 1], [2, 3])
-            for half in halves:
+            for half in HALVES:
                 bank = transpose_pairs(x_sb[0], half, psum_vector)
                 copy_pairs(nc.vector.tensor_copy, bank, x_bf16[0], half)
-            for half in halves:
+            for half in HALVES:
                 copy_pairs(nc.scalar.copy, transpose_pairs(w_sb, half, psum_scalar), w_bf16, half)
             x_mx[0] = quantise(x_bf16[0][:], per_batch, "x")
             w_mx.extend(quantise(w_bf16[:], const, "w"))

@@ -21,6 +21,7 @@ ROUNDS = BATCH * HEADS
 OUTPUT_LAG = 3
 TRANSPOSE_LEAD = 2
 LOAD_LEAD = 3
+ATTN_TILES = 3
 X_ROUND = 1
 HALVES = ([0, 1], [2, 3])
 FAR = 2.0**20
@@ -86,7 +87,7 @@ def tile_multiscaleretention_pa_t_kernel(tc, q, k, x, W_v, out):
         make_identity(nc, ident_f32[:])
 
         attn_bf16 = []
-        for n in range(2):
+        for n in range(ATTN_TILES):
             zeroed = const.tile([P, TOKENS, PACK], BF16, name="attn_bf16_%d" % n, align_bytes=64)
             nc.vector.memset(zeroed[:], 0.0)
             attn_bf16.append(zeroed)
@@ -185,7 +186,7 @@ def tile_multiscaleretention_pa_t_kernel(tc, q, k, x, W_v, out):
 
         def apply_decay(r, i):
             nc.vector.tensor_tensor(
-                out=attn_bf16[r % 2][:, block(i), 0 : i + 1],
+                out=attn_bf16[r % ATTN_TILES][:, block(i), 0 : i + 1],
                 in0=s_ps[r, i][:, 0 : i + 1, :].rearrange("p j t -> p t j"),
                 in1=decay[r % HEADS][:, :, BLOCKS - 1 - i : BLOCKS],
                 op=mybir.AluOpType.mult,
@@ -201,7 +202,7 @@ def tile_multiscaleretention_pa_t_kernel(tc, q, k, x, W_v, out):
 
         def first_block_decay(r):
             nc.gpsimd.tensor_tensor(
-                out=attn_bf16[r % 2][:, block(0), 0],
+                out=attn_bf16[r % ATTN_TILES][:, block(0), 0],
                 in0=s0_sb[r][:],
                 in1=decay[r % HEADS][:, :, BLOCKS - 1],
                 op=mybir.AluOpType.mult,
@@ -209,7 +210,7 @@ def tile_multiscaleretention_pa_t_kernel(tc, q, k, x, W_v, out):
 
         def quantise_attn(r):
             if r >= 0:
-                a_mx[r] = quantise(attn_bf16[r % 2][:].rearrange("p t j -> p (t j)"), waiting, "a")
+                a_mx[r] = quantise(attn_bf16[r % ATTN_TILES][:].rearrange("p t j -> p (t j)"), waiting, "a")
 
         def output(r):
             if r < 0:

@@ -17,13 +17,7 @@ TOKENS = 512
 CHANNELS = 512
 HEADS = CHANNELS // P
 BLOCKS = TOKENS // P
-ROUNDS = BATCH * HEADS
-OUTPUT_LAG = 3
-TRANSPOSE_LEAD = 2
-LOAD_LEAD = 3
-ATTN_TILES = 3
-X_ROUND = 1
-HALVES = ([0, 1], [2, 3])
+SLOTS = BATCH * HEADS // 2
 FAR = 2.0**20
 
 FLOPS = 3 * 2 * BATCH * TOKENS * TOKENS * CHANNELS
@@ -33,36 +27,64 @@ def block(n):
     return slice(P * n, P * (n + 1))
 
 
+def pair_block(n):
+    return slice(2 * P * n, 2 * P * (n + 1))
+
+
 def tile_multiscaleretention_pa_t_kernel(tc, q, k, x, W_v, out):
     nc = tc.nc
     with ExitStack() as ctx:
         const = ctx.enter_context(tc.tile_pool(name="const", bufs=1))
         inputs = ctx.enter_context(tc.tile_pool(name="inputs", bufs=BATCH))
         per_batch = ctx.enter_context(tc.tile_pool(name="per_batch", bufs=2))
-        per_round = ctx.enter_context(tc.tile_pool(name="per_round", bufs=3))
-        transposed = ctx.enter_context(tc.tile_pool(name="transposed", bufs=TRANSPOSE_LEAD + 1))
-        waiting = ctx.enter_context(tc.tile_pool(name="waiting", bufs=OUTPUT_LAG + 1))
+        per_slot = ctx.enter_context(tc.tile_pool(name="per_slot", bufs=3))
+        transposed = ctx.enter_context(tc.tile_pool(name="transposed", bufs=6))
         psum_scalar = ctx.enter_context(tc.psum_pool(name="psum_scalar", bufs=4))
         psum_vector = ctx.enter_context(tc.psum_pool(name="psum_vector", bufs=4))
         ctx.enter_context(tc.manual_schedule())
 
-        def load_rows(pool, matrix, name):
-            rows = pool.tile([P, BLOCKS, CHANNELS], BF16, name=name, tag=name)
-            nc.sync.dma_start(out=rows[:], in_=matrix.rearrange("(r p) c -> p r c", p=P))
-            return rows
-
         k_sb, q_sb, x_sb = {}, {}, {}
+
+        def new_rows(pool, name):
+            return pool.tile([P, BLOCKS, CHANNELS], BF16, name=name, tag=name)
+
+        def load(rows, matrix, columns):
+            nc.sync.dma_start(
+                out=rows[:, :, columns],
+                in_=matrix[:, columns].rearrange("(r p) c -> p r c", p=P),
+            )
+
+        def load_half(rows, matrix, half):
+            nc.sync.dma_start(
+                out=rows[:, 2 * half : 2 * half + 2, :],
+                in_=matrix[pair_block(half), :].rearrange("(r p) c -> p r c", p=P),
+            )
+
+        every = slice(0, CHANNELS)
 
         def load_batch(b):
             if b < BATCH:
-                k_sb[b] = load_rows(inputs, k[b], "k_sb")
-                q_sb[b] = load_rows(inputs, q[b], "q_sb")
-                x_sb[b] = load_rows(inputs, x[b], "x_sb")
+                for store, matrix, name in ((k_sb, k, "k_sb"), (q_sb, q, "q_sb")):
+                    store[b] = new_rows(inputs, name)
+                    load(store[b], matrix[b], every)
 
-        load_batch(0)
-        w_sb = load_rows(const, W_v, "w_sb")
-        for b in range(1, LOAD_LEAD):
-            load_batch(b)
+        def load_x(b):
+            if b < BATCH:
+                x_sb[b] = new_rows(inputs, "x_sb")
+                load(x_sb[b], x[b], every)
+
+        for store, name in ((k_sb, "k_sb"), (q_sb, "q_sb"), (x_sb, "x_sb")):
+            store[0] = new_rows(inputs, name)
+        w_sb = new_rows(const, "w_sb")
+        load_half(x_sb[0], x[0], 0)
+        load_half(x_sb[0], x[0], 1)
+        load(w_sb, W_v, every)
+        for pair in range(2):
+            load(k_sb[0], k[0], pair_block(pair))
+            load(q_sb[0], q[0], pair_block(pair))
+        load_x(1)
+        load_batch(1)
+        load_x(2)
 
         distance = const.tile([P, P, BLOCKS], F32, name="distance")
         nc.gpsimd.iota(
@@ -87,23 +109,21 @@ def tile_multiscaleretention_pa_t_kernel(tc, q, k, x, W_v, out):
         make_identity(nc, ident_f32[:])
 
         attn_bf16 = []
-        for n in range(ATTN_TILES):
-            zeroed = const.tile([P, TOKENS, PACK], BF16, name="attn_bf16_%d" % n, align_bytes=64)
+        for n in range(2):
+            zeroed = const.tile([P, 2, TOKENS, PACK], BF16, name="attn_bf16_%d" % n, align_bytes=64)
             nc.vector.memset(zeroed[:], 0.0)
             attn_bf16.append(zeroed)
 
-        decay = []
+        decay = const.tile([P, HEADS, P, BLOCKS], F32, name="decay")
 
         def make_decay(h):
-            table = const.tile([P, P, BLOCKS], F32, name="decay_%d" % h)
             nc.scalar.activation(
-                out=table[:],
+                out=decay[:, h],
                 in_=distance[:],
                 func=mybir.ActivationFunctionType.Exp,
                 scale=math.log(1.0 - 2.0 ** (-5 - h)),
                 bias=-0.5 * math.log(P),
             )
-            decay.append(table)
 
         def quantise(grouped, pool, name):
             n = grouped.shape[1] // PACK
@@ -115,179 +135,247 @@ def tile_multiscaleretention_pa_t_kernel(tc, q, k, x, W_v, out):
         def new_grouped(pool, name):
             return pool.tile([P, TOKENS * PACK], BF16, name=name, align_bytes=64)
 
-        def transpose_pairs(rows, places, psum):
-            bank = psum.tile([P, 2, len(places) * P], F32, name="pairs_ps", tag="bank")
-            for n, r in enumerate(places):
-                row_pairs = rows[:, r, :].bitcast(F32)
+        def transpose_pairs(rows, half):
+            bank = psum_scalar.tile([P, 2, 2 * P], F32, name="pairs_ps", tag="bank")
+            for n in range(2):
+                row_pairs = rows[:, 2 * half + n, :].bitcast(F32)
                 for u in range(2):
                     nc.tensor.transpose(bank[:, u, block(n)], row_pairs[:, block(u)], ident_f32[:])
             return bank
 
-        def copy_pairs(copy, bank, grouped, places):
+        def copy_pairs(copy, bank, grouped, half):
             pairs = grouped[:].bitcast(F32).rearrange("p (n u) -> p n u", u=2)
             copy(
-                out=pairs[:, P * places[0] : P * (places[-1] + 1), :],
+                out=pairs[:, 2 * P * half : 2 * P * (half + 1), :],
                 in_=bank[:].rearrange("p u n -> p n u"),
             )
 
         x_bf16, x_mx, v_bf16, v_mx = {}, {}, {}, {}
 
-        def project_values(r):
-            if r >= ROUNDS:
+        def transpose_x(b, half):
+            if b >= BATCH:
                 return
-            b, h = divmod(r, HEADS)
+            if half == 0:
+                x_bf16[b] = new_grouped(per_batch, "x_bf16")
+            copy_pairs(nc.scalar.copy, transpose_pairs(x_sb[b], half), x_bf16[b], half)
+
+        def quantise_x(b):
+            if b < BATCH:
+                x_mx[b] = quantise(x_bf16[b][:], per_batch, "x")
+
+        def project_values(b, h):
+            if b >= BATCH:
+                return
             v_ps = psum_scalar.tile([P, BLOCKS, P], F32, name="v_ps", tag="bank")
             for j in range(BLOCKS):
                 nc.tensor.matmul_mx(
                     out=v_ps[:, j, :],
                     lhsT=x_mx[b][0][:, block(j)].bitcast(FP8X4),
                     lhsT_scale=x_mx[b][1][:, block(j)],
-                    rhs=w_mx[0][:, block(h)].bitcast(FP8X4),
-                    rhs_scale=w_mx[1][:, block(h)],
+                    rhs=w_mx[0][0][:, block(h)].bitcast(FP8X4),
+                    rhs_scale=w_mx[0][1][:, block(h)],
                     start=True,
                     stop=True,
                 )
-            if r % 2 == 0:
-                v_bf16[r // 2] = per_round.tile([P, 2, P, PACK], BF16, name="v_bf16", align_bytes=64)
-            nc.scalar.copy(out=v_bf16[r // 2][:, r % 2], in_=v_ps[:].rearrange("p j c -> p c j"))
+            if h == 0:
+                v_bf16[b] = per_batch.tile([P, HEADS, P, PACK], BF16, name="v_bf16", align_bytes=64)
+            nc.scalar.copy(out=v_bf16[b][:, h], in_=v_ps[:].rearrange("p j c -> p c j"))
 
-        def quantise_values(pair):
-            grouped = v_bf16[pair][:].rearrange("p n c j -> p (n c j)")
-            v_mx[pair] = quantise(grouped, waiting, "v")
+        def quantise_v(b):
+            v_mx[b] = quantise(v_bf16[b][:].rearrange("p h c j -> p (h c j)"), per_batch, "v")
 
         kq, s_ps, s0_sb, a_mx = {}, {}, {}, {}
 
-        def head_channels_to_partitions(r):
-            if r >= ROUNDS:
+        def transpose_kq(s, n):
+            if s >= SLOTS:
                 return
-            b, h = divmod(r, HEADS)
+            b, h = s // 2, 2 * (s % 2) + n
             kq_ps = psum_scalar.tile([P, 2, TOKENS], BF16, name="kq_ps", tag="bank")
             for side, rows in enumerate((k_sb[b], q_sb[b])):
-                for n in range(BLOCKS):
-                    nc.tensor.transpose(kq_ps[:, side, block(n)], rows[:, n, block(h)], ident_bf16[:])
-            kq[r] = transposed.tile([P, 2, TOKENS], BF16, name="kq")
-            nc.scalar.copy(out=kq[r][:], in_=kq_ps[:])
+                for i in range(BLOCKS):
+                    nc.tensor.transpose(kq_ps[:, side, block(i)], rows[:, i, block(h)], ident_bf16[:])
+            kq[s, n] = transposed.tile([P, 2, TOKENS], BF16, name="kq")
+            nc.scalar.copy(out=kq[s, n][:], in_=kq_ps[:])
 
-        def score_blocks(r, bank, places):
-            for n, (i, j) in enumerate(places):
-                nc.tensor.matmul(
-                    out=bank[:, n, :],
-                    lhsT=kq[r][:, 0, block(j)],
-                    rhs=kq[r][:, 1, block(i)],
-                    start=True,
-                    stop=True,
-                )
-
-        def scores(r, i):
-            if r >= ROUNDS:
-                return
-            s_ps[r, i] = psum_vector.tile([P, BLOCKS, P], F32, name="s_ps", tag="bank")
-            score_blocks(r, s_ps[r, i], [(i, j) for j in range(i + 1)])
-
-        def apply_decay(r, i):
-            nc.vector.tensor_tensor(
-                out=attn_bf16[r % ATTN_TILES][:, block(i), 0 : i + 1],
-                in0=s_ps[r, i][:, 0 : i + 1, :].rearrange("p j t -> p t j"),
-                in1=decay[r % HEADS][:, :, BLOCKS - 1 - i : BLOCKS],
-                op=mybir.AluOpType.mult,
+        def score_block(bank, s, n, i, j):
+            nc.tensor.matmul(
+                out=bank,
+                lhsT=kq[s, n][:, 0, block(j)],
+                rhs=kq[s, n][:, 1, block(i)],
+                start=True,
+                stop=True,
             )
 
-        def first_block_scores(r):
-            if r >= ROUNDS:
-                return
-            s0_ps = psum_scalar.tile([P, 1, P], F32, name="s0_ps", tag="bank")
-            score_blocks(r, s0_ps, [(0, 0)])
-            s0_sb[r] = per_round.tile([P, P], F32, name="s0_sb")
-            nc.scalar.copy(out=s0_sb[r][:], in_=s0_ps[:, 0, :])
+        USES = ((2, 0), (3, 0), (1, None), (2, 1), (3, 1))
 
-        def first_block_decay(r):
+        def scores(u):
+            s, use = divmod(u, len(USES))
+            if s >= SLOTS:
+                return
+            i, n = USES[use]
+            if n is None:
+                s_ps[u] = psum_vector.tile([P, 2, 2, P], F32, name="s_ps", tag="bank")
+                for m in range(2):
+                    for j in range(2):
+                        score_block(s_ps[u][:, m, j, :], s, m, i, j)
+            else:
+                s_ps[u] = psum_vector.tile([P, BLOCKS, P], F32, name="s_ps", tag="bank")
+                for j in range(i + 1):
+                    score_block(s_ps[u][:, j, :], s, n, i, j)
+
+        def apply_decay(u):
+            s, use = divmod(u, len(USES))
+            i, n = USES[use]
+            attn, h = attn_bf16[s % 2], 2 * (s % 2)
+            if n is None:
+                out_, in0 = attn[:, :, block(i), 0 : i + 1], s_ps[u][:].rearrange("p n j t -> p n t j")
+                in1 = decay[:, h : h + 2, :, BLOCKS - 1 - i : BLOCKS]
+            else:
+                out_, in0 = attn[:, n, block(i), 0 : i + 1], s_ps[u][:, 0 : i + 1, :].rearrange("p j t -> p t j")
+                in1 = decay[:, h + n, :, BLOCKS - 1 - i : BLOCKS]
+            nc.vector.tensor_tensor(out=out_, in0=in0, in1=in1, op=mybir.AluOpType.mult)
+
+        def first_block_scores(s):
+            if s >= SLOTS:
+                return
+            s0_ps = psum_scalar.tile([P, 2, P], F32, name="s0_ps", tag="bank")
+            for n in range(2):
+                score_block(s0_ps[:, n, :], s, n, 0, 0)
+            s0_sb[s] = per_slot.tile([P, 2, P], F32, name="s0_sb")
+            nc.scalar.copy(out=s0_sb[s][:], in_=s0_ps[:])
+
+        def first_block_decay(s):
+            if s >= SLOTS:
+                return
+            h = 2 * (s % 2)
             nc.gpsimd.tensor_tensor(
-                out=attn_bf16[r % ATTN_TILES][:, block(0), 0],
-                in0=s0_sb[r][:],
-                in1=decay[r % HEADS][:, :, BLOCKS - 1],
+                out=attn_bf16[s % 2][:, :, block(0), 0],
+                in0=s0_sb[s][:],
+                in1=decay[:, h : h + 2, :, BLOCKS - 1],
                 op=mybir.AluOpType.mult,
             )
 
-        def quantise_attn(r):
-            if r >= 0:
-                a_mx[r] = quantise(attn_bf16[r % ATTN_TILES][:].rearrange("p t j -> p (t j)"), waiting, "a")
+        def quantise_attn(s):
+            if s >= 0:
+                a_mx[s] = quantise(attn_bf16[s % 2][:].rearrange("p n t j -> p (n t j)"), per_slot, "a")
 
-        def output(r):
-            if r < 0:
-                return
-            b, h = divmod(r, HEADS)
-            y_ps = psum_scalar.tile([P, BLOCKS, P], F32, name="y_ps", tag="bank")
-            for i in range(BLOCKS):
-                nc.tensor.matmul_mx(
-                    out=y_ps[:, i, :],
-                    lhsT=a_mx[r][0][:, block(i)].bitcast(FP8X4),
-                    lhsT_scale=a_mx[r][1][:, block(i)],
-                    rhs=v_mx[r // 2][0][:, block(r % 2)].bitcast(FP8X4),
-                    rhs_scale=v_mx[r // 2][1][:, block(r % 2)],
-                    start=True,
-                    stop=True,
-                )
-            y_sb = per_round.tile([P, BLOCKS, P], F32, name="y_sb")
-            nc.scalar.copy(out=y_sb[:], in_=y_ps[:])
-            nc.sync.dma_start(
-                out=out[b][:, block(h)].rearrange("(i p) c -> p i c", p=P), in_=y_sb[:]
+        def attend(out_, words, scales, b, h):
+            nc.tensor.matmul_mx(
+                out=out_,
+                lhsT=words.bitcast(FP8X4),
+                lhsT_scale=scales,
+                rhs=v_mx[b][0][:, block(h)].bitcast(FP8X4),
+                rhs_scale=v_mx[b][1][:, block(h)],
+                start=True,
+                stop=True,
             )
 
-        def transpose_x(b):
-            x_bf16[b] = new_grouped(per_batch, "x_bf16")
-            banks = [transpose_pairs(x_sb[b], half, psum_scalar) for half in HALVES]
-            for half, bank in zip(HALVES, banks):
-                copy_pairs(nc.scalar.copy, bank, x_bf16[b], half)
+        def output(s):
+            if s < 0:
+                return
+            b, h = s // 2, 2 * (s % 2)
+            y_sb = per_slot.tile([P, BLOCKS, 2, P], F32, name="y_sb")
+            for n in range(2):
+                y_ps = psum_scalar.tile([P, BLOCKS, P], F32, name="y_ps", tag="bank")
+                for i in range(BLOCKS):
+                    at = block(BLOCKS * n + i)
+                    attend(y_ps[:, i, :], a_mx[s][0][:, at], a_mx[s][1][:, at], b, h + n)
+                nc.scalar.copy(out=y_sb[:, :, n, :], in_=y_ps[:])
+            nc.sync.dma_start(
+                out=out[b][:, pair_block(s % 2)].rearrange("(i p) (n c) -> p i n c", p=P, n=2),
+                in_=y_sb[:],
+            )
 
-        def head_round(r):
-            b, h = divmod(r, HEADS)
-            if h == 0:
-                load_batch(b + LOAD_LEAD)
-            first_block_decay(r)
-            for i in range(1, BLOCKS):
-                apply_decay(r, i)
-            if r == 0:
-                first_x_and_w()
-            scores(r + 1, 1)
-            first_block_scores(r + 1)
-            head_channels_to_partitions(r + TRANSPOSE_LEAD)
-            if h == X_ROUND and b + 1 < BATCH:
-                transpose_x(b + 1)
-            scores(r + 1, 2)
-            output(r - OUTPUT_LAG)
-            if h == 2 and b + 1 < BATCH:
-                x_mx[b + 1] = quantise(x_bf16[b + 1][:], per_batch, "x")
-            scores(r + 1, 3)
-            if r == 0:
-                project_values(0)
-            project_values(r + 1)
-            if r % 2 == 0 and r > 0:
-                quantise_values(r // 2 - 1)
-            quantise_attn(r - 1)
+        def quantise_part(s, n, i0, i1):
+            part = attn_bf16[s % 2][:, n, P * i0 : P * i1, :].rearrange("p t j -> p (t j)")
+            return quantise(part, const, "last_%d_%d" % (n, i0))
+
+        def output_part(s, n, i0, i1, part, copy):
+            b, h = s // 2, 2 * (s % 2) + n
+            y_sb = const.tile([P, i1 - i0, P], F32, name="last_y_%d_%d" % (n, i0))
+            y_ps = psum_scalar.tile([P, i1 - i0, P], F32, name="y_ps", tag="bank")
+            for i in range(i1 - i0):
+                attend(y_ps[:, i, :], part[0][:, block(i)], part[1][:, block(i)], b, h)
+            copy(out=y_sb[:], in_=y_ps[:])
+            nc.sync.dma_start(
+                out=out[b][P * i0 : P * i1, block(h)].rearrange("(i p) c -> p i c", p=P), in_=y_sb[:]
+            )
+
+        w_mx = []
+
+        AHEAD = 3
+
+        def slot(s):
+            b, odd = divmod(s, 2)
+            u = len(USES) * s
+            if not odd:
+                load_batch(b + 2)
+                load_x(b + 3)
+            apply_decay(u)
+            scores(u + AHEAD)
+            if s == 1:
+                quantise_x(1)
+            if odd:
+                quantise_v(b)
+            elif s > 0:
+                quantise_x(b + 1)
+            quantise_attn(s - 1)
+            if s > 0:
+                vb, vh = divmod(s + 1, 2)
+                project_values(vb, 2 * vh)
+                project_values(vb, 2 * vh + 1)
+            else:
+                project_values(0, 2)
+                project_values(0, 3)
+            first_block_scores(s + 1)
+            if s == 0:
+                transpose_x(1, 0)
+                transpose_x(1, 1)
+            elif s == 1:
+                transpose_x(2, 0)
+                transpose_x(2, 1)
+            else:
+                transpose_x(b + 2, odd)
+            apply_decay(u + 1)
+            scores(u + 1 + AHEAD)
+            first_block_decay(s + 1)
+            output(s - 1)
+            apply_decay(u + 2)
+            scores(u + 2 + AHEAD)
+            transpose_kq(s + 2, 0)
+            transpose_kq(s + 2, 1)
+            apply_decay(u + 3)
+            scores(u + 3 + AHEAD)
+            if s == SLOTS - 1:
+                first = quantise_part(s, 0, 0, BLOCKS)
+            apply_decay(u + 4)
+            scores(u + 4 + AHEAD)
+            if s == SLOTS - 1:
+                second = quantise_part(s, 1, 0, 2)
+                third = quantise_part(s, 1, 2, BLOCKS)
+                output_part(s, 0, 0, BLOCKS, first, nc.scalar.copy)
+                output_part(s, 1, 0, 2, second, nc.vector.tensor_copy)
+                output_part(s, 1, 2, BLOCKS, third, nc.scalar.copy)
 
         for h in range(HEADS):
             make_decay(h)
-        head_channels_to_partitions(0)
-        head_channels_to_partitions(1)
-        for i in range(1, BLOCKS):
-            scores(0, i)
-        first_block_scores(0)
         w_bf16 = new_grouped(const, "w_bf16")
         x_bf16[0] = new_grouped(per_batch, "x_bf16")
-        w_mx = []
-
-        def first_x_and_w():
-            for half in HALVES:
-                bank = transpose_pairs(x_sb[0], half, psum_vector)
-                copy_pairs(nc.vector.tensor_copy, bank, x_bf16[0], half)
-            for half in HALVES:
-                copy_pairs(nc.scalar.copy, transpose_pairs(w_sb, half, psum_scalar), w_bf16, half)
-            x_mx[0] = quantise(x_bf16[0][:], per_batch, "x")
-            w_mx.extend(quantise(w_bf16[:], const, "w"))
-
-        for r in range(ROUNDS):
-            head_round(r)
-        quantise_values(ROUNDS // 2 - 1)
-        quantise_attn(ROUNDS - 1)
-        for r in range(ROUNDS - OUTPUT_LAG, ROUNDS):
-            output(r)
+        for rows, grouped in ((x_sb[0], x_bf16[0]), (w_sb, w_bf16)):
+            for half, copy in enumerate((nc.scalar.copy, nc.vector.tensor_copy)):
+                copy_pairs(copy, transpose_pairs(rows, half), grouped, half)
+        transpose_kq(0, 0)
+        quantise_x(0)
+        w_mx.append(quantise(w_bf16[:], const, "w"))
+        transpose_kq(0, 1)
+        scores(0)
+        scores(1)
+        project_values(0, 0)
+        project_values(0, 1)
+        scores(2)
+        transpose_kq(1, 0)
+        first_block_scores(0)
+        first_block_decay(0)
+        transpose_kq(1, 1)
+        for s in range(SLOTS):
+            slot(s)

@@ -86,6 +86,8 @@ def tile_multiscaleretention_pa_t_kernel(tc, q, k, x, W_v, out):
         load_batch(1)
         load_x(2)
 
+        ident_f32 = const.tile([P, P], F32, name="ident_f32")
+        make_identity(nc, ident_f32[:])
         distance = const.tile([P, P, BLOCKS], F32, name="distance")
         nc.gpsimd.iota(
             distance[:],
@@ -105,13 +107,12 @@ def tile_multiscaleretention_pa_t_kernel(tc, q, k, x, W_v, out):
         )
         ident_bf16 = const.tile([P, P], BF16, name="ident_bf16")
         make_identity(nc, ident_bf16[:])
-        ident_f32 = const.tile([P, P], F32, name="ident_f32")
-        make_identity(nc, ident_f32[:])
 
         attn_bf16 = []
         for n in range(2):
             zeroed = const.tile([P, 2, TOKENS, PACK], BF16, name="attn_bf16_%d" % n, align_bytes=64)
-            nc.vector.memset(zeroed[:], 0.0)
+            above = zeroed[:].rearrange("p n t j -> p n (t j)").bitcast(F32)
+            nc.vector.memset(above[:, :, 0 : 2 * P * (BLOCKS - 1)], 0.0)
             attn_bf16.append(zeroed)
 
         decay = const.tile([P, HEADS, P, BLOCKS], F32, name="decay")
@@ -184,7 +185,7 @@ def tile_multiscaleretention_pa_t_kernel(tc, q, k, x, W_v, out):
         def quantise_v(b):
             v_mx[b] = quantise(v_bf16[b][:].rearrange("p h c j -> p (h c j)"), per_batch, "v")
 
-        kq, s_ps, s0_sb, a_mx = {}, {}, {}, {}
+        kq, s_ps, side_sb, a_mx = {}, {}, {}, {}
 
         def transpose_kq(s, n):
             if s >= SLOTS:
@@ -193,7 +194,13 @@ def tile_multiscaleretention_pa_t_kernel(tc, q, k, x, W_v, out):
             kq_ps = psum_scalar.tile([P, 2, TOKENS], BF16, name="kq_ps", tag="bank")
             for side, rows in enumerate((k_sb[b], q_sb[b])):
                 for i in range(BLOCKS):
-                    nc.tensor.transpose(kq_ps[:, side, block(i)], rows[:, i, block(h)], ident_bf16[:])
+                    nc.tensor.matmul(
+                        out=kq_ps[:, side, block(i)],
+                        lhsT=rows[:, i, block(h)],
+                        rhs=ident_bf16[:],
+                        start=True,
+                        stop=True,
+                    )
             kq[s, n] = transposed.tile([P, 2, TOKENS], BF16, name="kq")
             nc.scalar.copy(out=kq[s, n][:], in_=kq_ps[:])
 
@@ -206,52 +213,50 @@ def tile_multiscaleretention_pa_t_kernel(tc, q, k, x, W_v, out):
                 stop=True,
             )
 
-        USES = ((2, 0), (3, 0), (1, None), (2, 1), (3, 1))
+        USES = ((2, 0), (3, 0), (1, 0), (2, 1), (3, 1))
 
         def scores(u):
             s, use = divmod(u, len(USES))
             if s >= SLOTS:
                 return
             i, n = USES[use]
-            if n is None:
-                s_ps[u] = psum_vector.tile([P, 2, 2, P], F32, name="s_ps", tag="bank")
-                for m in range(2):
-                    for j in range(2):
-                        score_block(s_ps[u][:, m, j, :], s, m, i, j)
-            else:
-                s_ps[u] = psum_vector.tile([P, BLOCKS, P], F32, name="s_ps", tag="bank")
-                for j in range(i + 1):
-                    score_block(s_ps[u][:, j, :], s, n, i, j)
+            s_ps[u] = psum_vector.tile([P, BLOCKS, P], F32, name="s_ps", tag="bank")
+            for j in range(i + 1):
+                score_block(s_ps[u][:, j, :], s, n, i, j)
 
         def apply_decay(u):
             s, use = divmod(u, len(USES))
             i, n = USES[use]
-            attn, h = attn_bf16[s % 2], 2 * (s % 2)
-            if n is None:
-                out_, in0 = attn[:, :, block(i), 0 : i + 1], s_ps[u][:].rearrange("p n j t -> p n t j")
-                in1 = decay[:, h : h + 2, :, BLOCKS - 1 - i : BLOCKS]
-            else:
-                out_, in0 = attn[:, n, block(i), 0 : i + 1], s_ps[u][:, 0 : i + 1, :].rearrange("p j t -> p t j")
-                in1 = decay[:, h + n, :, BLOCKS - 1 - i : BLOCKS]
-            nc.vector.tensor_tensor(out=out_, in0=in0, in1=in1, op=mybir.AluOpType.mult)
+            nc.vector.tensor_tensor(
+                out=attn_bf16[s % 2][:, n, block(i), 0 : i + 1],
+                in0=s_ps[u][:, 0 : i + 1, :].rearrange("p j t -> p t j"),
+                in1=decay[:, 2 * (s % 2) + n, :, BLOCKS - 1 - i : BLOCKS],
+                op=mybir.AluOpType.mult,
+            )
 
-        def first_block_scores(s):
+        def side_scores(s):
             if s >= SLOTS:
                 return
-            s0_ps = psum_scalar.tile([P, 2, P], F32, name="s0_ps", tag="bank")
-            for n in range(2):
-                score_block(s0_ps[:, n, :], s, n, 0, 0)
-            s0_sb[s] = per_slot.tile([P, 2, P], F32, name="s0_sb")
-            nc.scalar.copy(out=s0_sb[s][:], in_=s0_ps[:])
+            bank = psum_scalar.tile([P, 4, P], F32, name="side_ps", tag="bank")
+            for place, (n, i, j) in enumerate(((0, 0, 0), (1, 0, 0), (1, 1, 0), (1, 1, 1))):
+                score_block(bank[:, place, :], s, n, i, j)
+            side_sb[s] = per_slot.tile([P, 4, P], F32, name="side_sb")
+            nc.scalar.copy(out=side_sb[s][:], in_=bank[:])
 
-        def first_block_decay(s):
+        def side_decay(s):
             if s >= SLOTS:
                 return
             h = 2 * (s % 2)
             nc.gpsimd.tensor_tensor(
                 out=attn_bf16[s % 2][:, :, block(0), 0],
-                in0=s0_sb[s][:],
+                in0=side_sb[s][:, 0:2, :],
                 in1=decay[:, h : h + 2, :, BLOCKS - 1],
+                op=mybir.AluOpType.mult,
+            )
+            nc.gpsimd.tensor_tensor(
+                out=attn_bf16[s % 2][:, 1, block(1), 0:2],
+                in0=side_sb[s][:, 2:4, :].rearrange("p j t -> p t j"),
+                in1=decay[:, h + 1, :, BLOCKS - 2 : BLOCKS],
                 op=mybir.AluOpType.mult,
             )
 
@@ -270,21 +275,24 @@ def tile_multiscaleretention_pa_t_kernel(tc, q, k, x, W_v, out):
                 stop=True,
             )
 
-        def output(s):
+        y_sb = {}
+
+        def output(s, n):
             if s < 0:
                 return
             b, h = s // 2, 2 * (s % 2)
-            y_sb = per_slot.tile([P, BLOCKS, 2, P], F32, name="y_sb")
-            for n in range(2):
-                y_ps = psum_scalar.tile([P, BLOCKS, P], F32, name="y_ps", tag="bank")
-                for i in range(BLOCKS):
-                    at = block(BLOCKS * n + i)
-                    attend(y_ps[:, i, :], a_mx[s][0][:, at], a_mx[s][1][:, at], b, h + n)
-                nc.scalar.copy(out=y_sb[:, :, n, :], in_=y_ps[:])
-            nc.sync.dma_start(
-                out=out[b][:, pair_block(s % 2)].rearrange("(i p) (n c) -> p i n c", p=P, n=2),
-                in_=y_sb[:],
-            )
+            if n == 0:
+                y_sb[s] = per_slot.tile([P, BLOCKS, 2, P], F32, name="y_sb")
+            y_ps = psum_scalar.tile([P, BLOCKS, P], F32, name="y_ps", tag="bank")
+            for i in range(BLOCKS):
+                at = block(BLOCKS * n + i)
+                attend(y_ps[:, i, :], a_mx[s][0][:, at], a_mx[s][1][:, at], b, h + n)
+            nc.scalar.copy(out=y_sb[s][:, :, n, :], in_=y_ps[:])
+            if n == 1:
+                nc.sync.dma_start(
+                    out=out[b][:, pair_block(s % 2)].rearrange("(i p) (n c) -> p i n c", p=P, n=2),
+                    in_=y_sb[s][:],
+                )
 
         def quantise_part(s, n, i0, i1):
             part = attn_bf16[s % 2][:, n, P * i0 : P * i1, :].rearrange("p t j -> p (t j)")
@@ -292,13 +300,13 @@ def tile_multiscaleretention_pa_t_kernel(tc, q, k, x, W_v, out):
 
         def output_part(s, n, i0, i1, part, copy):
             b, h = s // 2, 2 * (s % 2) + n
-            y_sb = const.tile([P, i1 - i0, P], F32, name="last_y_%d_%d" % (n, i0))
+            last_y = const.tile([P, i1 - i0, P], F32, name="last_y_%d_%d" % (n, i0))
             y_ps = psum_scalar.tile([P, i1 - i0, P], F32, name="y_ps", tag="bank")
             for i in range(i1 - i0):
                 attend(y_ps[:, i, :], part[0][:, block(i)], part[1][:, block(i)], b, h)
-            copy(out=y_sb[:], in_=y_ps[:])
+            copy(out=last_y[:], in_=y_ps[:])
             nc.sync.dma_start(
-                out=out[b][P * i0 : P * i1, block(h)].rearrange("(i p) c -> p i c", p=P), in_=y_sb[:]
+                out=out[b][P * i0 : P * i1, block(h)].rearrange("(i p) c -> p i c", p=P), in_=last_y[:]
             )
 
         w_mx = []
@@ -308,11 +316,13 @@ def tile_multiscaleretention_pa_t_kernel(tc, q, k, x, W_v, out):
         def slot(s):
             b, odd = divmod(s, 2)
             u = len(USES) * s
+            last = s == SLOTS - 1
             if not odd:
                 load_batch(b + 2)
                 load_x(b + 3)
             apply_decay(u)
             scores(u + AHEAD)
+            transpose_kq(s + 1, 0)
             if s == 1:
                 quantise_x(1)
             if odd:
@@ -320,14 +330,13 @@ def tile_multiscaleretention_pa_t_kernel(tc, q, k, x, W_v, out):
             elif s > 0:
                 quantise_x(b + 1)
             quantise_attn(s - 1)
-            if s > 0:
-                vb, vh = divmod(s + 1, 2)
-                project_values(vb, 2 * vh)
-                project_values(vb, 2 * vh + 1)
-            else:
-                project_values(0, 2)
-                project_values(0, 3)
-            first_block_scores(s + 1)
+            side_scores(s)
+            side_decay(s)
+            transpose_kq(s + 1, 1)
+            vb, vh = divmod(s + 1, 2)
+            if s == 0:
+                vb, vh = 0, 1
+            project_values(vb, 2 * vh)
             if s == 0:
                 transpose_x(1, 0)
                 transpose_x(1, 1)
@@ -338,44 +347,41 @@ def tile_multiscaleretention_pa_t_kernel(tc, q, k, x, W_v, out):
                 transpose_x(b + 2, odd)
             apply_decay(u + 1)
             scores(u + 1 + AHEAD)
-            first_block_decay(s + 1)
-            output(s - 1)
+            project_values(vb, 2 * vh + 1)
             apply_decay(u + 2)
             scores(u + 2 + AHEAD)
-            transpose_kq(s + 2, 0)
-            transpose_kq(s + 2, 1)
+            output(s - 1, 0)
             apply_decay(u + 3)
             scores(u + 3 + AHEAD)
-            if s == SLOTS - 1:
+            if last:
                 first = quantise_part(s, 0, 0, BLOCKS)
+            output(s - 1, 1)
             apply_decay(u + 4)
             scores(u + 4 + AHEAD)
-            if s == SLOTS - 1:
+            if last:
                 second = quantise_part(s, 1, 0, 2)
                 third = quantise_part(s, 1, 2, BLOCKS)
                 output_part(s, 0, 0, BLOCKS, first, nc.scalar.copy)
                 output_part(s, 1, 0, 2, second, nc.vector.tensor_copy)
                 output_part(s, 1, 2, BLOCKS, third, nc.scalar.copy)
 
-        for h in range(HEADS):
-            make_decay(h)
         w_bf16 = new_grouped(const, "w_bf16")
         x_bf16[0] = new_grouped(per_batch, "x_bf16")
         for rows, grouped in ((x_sb[0], x_bf16[0]), (w_sb, w_bf16)):
             for half, copy in enumerate((nc.scalar.copy, nc.vector.tensor_copy)):
                 copy_pairs(copy, transpose_pairs(rows, half), grouped, half)
+        make_decay(0)
+        make_decay(1)
         transpose_kq(0, 0)
         quantise_x(0)
         w_mx.append(quantise(w_bf16[:], const, "w"))
         transpose_kq(0, 1)
+        make_decay(2)
+        make_decay(3)
         scores(0)
         scores(1)
+        scores(2)
         project_values(0, 0)
         project_values(0, 1)
-        scores(2)
-        transpose_kq(1, 0)
-        first_block_scores(0)
-        first_block_decay(0)
-        transpose_kq(1, 1)
         for s in range(SLOTS):
             slot(s)

@@ -2,7 +2,6 @@ import math
 from contextlib import ExitStack
 
 import concourse.mybir as mybir
-from concourse.masks import make_identity
 
 F32 = mybir.dt.float32
 BF16 = mybir.dt.bfloat16
@@ -19,6 +18,8 @@ HEADS = CHANNELS // P
 BLOCKS = TOKENS // P
 SLOTS = BATCH * HEADS // 2
 FAR = 2.0**20
+
+WARM_UP = 4
 
 FLOPS = 3 * 2 * BATCH * TOKENS * TOKENS * CHANNELS
 
@@ -76,18 +77,17 @@ def tile_multiscaleretention_pa_t_kernel(tc, q, k, x, W_v, out):
         for store, name in ((k_sb, "k_sb"), (q_sb, "q_sb"), (x_sb, "x_sb")):
             store[0] = new_rows(inputs, name)
         w_sb = new_rows(const, "w_sb")
+        load(k_sb[0], k[0], pair_block(0))
+        load(q_sb[0], q[0], pair_block(0))
         load_half(x_sb[0], x[0], 0)
         load_half(x_sb[0], x[0], 1)
         load(w_sb, W_v, every)
-        for pair in range(2):
-            load(k_sb[0], k[0], pair_block(pair))
-            load(q_sb[0], q[0], pair_block(pair))
+        load(k_sb[0], k[0], pair_block(1))
+        load(q_sb[0], q[0], pair_block(1))
         load_x(1)
         load_batch(1)
         load_x(2)
 
-        ident_f32 = const.tile([P, P], F32, name="ident_f32")
-        make_identity(nc, ident_f32[:])
         distance = const.tile([P, P, BLOCKS], F32, name="distance")
         nc.gpsimd.iota(
             distance[:],
@@ -96,6 +96,20 @@ def tile_multiscaleretention_pa_t_kernel(tc, q, k, x, W_v, out):
             channel_multiplier=-1,
             allow_small_or_imprecise_dtypes=True,
         )
+        zeros = const.tile([P, TOKENS], BF16, name="zeros")
+        nc.vector.memset(zeros[:].bitcast(F32), 0.0)
+        idents = []
+        for name, dtype in (("ident_bf16", BF16), ("ident_f32", F32)):
+            ident = const.tile([P, P], dtype, name=name)
+            nc.vector.tensor_scalar(
+                out=ident[:],
+                in0=distance[:, :, BLOCKS - 1],
+                scalar1=0.0,
+                scalar2=None,
+                op0=mybir.AluOpType.is_equal,
+            )
+            idents.append(ident)
+        ident_bf16, ident_f32 = idents
         nc.gpsimd.affine_select(
             out=distance[:, :, BLOCKS - 1],
             in_=distance[:, :, BLOCKS - 1],
@@ -105,8 +119,6 @@ def tile_multiscaleretention_pa_t_kernel(tc, q, k, x, W_v, out):
             base=0,
             channel_multiplier=-1,
         )
-        ident_bf16 = const.tile([P, P], BF16, name="ident_bf16")
-        make_identity(nc, ident_bf16[:])
 
         attn_bf16 = []
         for n in range(2):
@@ -153,18 +165,26 @@ def tile_multiscaleretention_pa_t_kernel(tc, q, k, x, W_v, out):
 
         x_bf16, x_mx, v_bf16, v_mx = {}, {}, {}, {}
 
-        def transpose_x(b, half):
+        x_banks = {}
+
+        def transpose_x(b, half, copy=nc.scalar.copy):
             if b >= BATCH:
                 return
             if half == 0:
                 x_bf16[b] = new_grouped(per_batch, "x_bf16")
-            copy_pairs(nc.scalar.copy, transpose_pairs(x_sb[b], half), x_bf16[b], half)
+            x_banks[b, half] = transpose_pairs(x_sb[b], half)
+            if copy:
+                copy_x(copy, b, half)
+
+        def copy_x(copy, b, half):
+            if b < BATCH:
+                copy_pairs(copy, x_banks[b, half], x_bf16[b], half)
 
         def quantise_x(b):
             if b < BATCH:
                 x_mx[b] = quantise(x_bf16[b][:], per_batch, "x")
 
-        def project_values(b, h):
+        def project_values(b, h, copy=nc.scalar.copy):
             if b >= BATCH:
                 return
             v_ps = psum_scalar.tile([P, BLOCKS, P], F32, name="v_ps", tag="bank")
@@ -180,7 +200,7 @@ def tile_multiscaleretention_pa_t_kernel(tc, q, k, x, W_v, out):
                 )
             if h == 0:
                 v_bf16[b] = per_batch.tile([P, HEADS, P, PACK], BF16, name="v_bf16", align_bytes=64)
-            nc.scalar.copy(out=v_bf16[b][:, h], in_=v_ps[:].rearrange("p j c -> p c j"))
+            copy(out=v_bf16[b][:, h], in_=v_ps[:].rearrange("p j c -> p c j"))
 
         def quantise_v(b):
             v_mx[b] = quantise(v_bf16[b][:].rearrange("p h c j -> p (h c j)"), per_batch, "v")
@@ -313,6 +333,32 @@ def tile_multiscaleretention_pa_t_kernel(tc, q, k, x, W_v, out):
 
         AHEAD = 3
 
+        def first_slot():
+            apply_decay(0)
+            scores(AHEAD)
+            copy_pairs(nc.vector.tensor_copy, first_banks[1], x_bf16[0], 1)
+            transpose_kq(1, 0)
+            apply_decay(1)
+            scores(1 + AHEAD)
+            copy_pairs(nc.vector.tensor_copy, first_banks[3], w_bf16, 1)
+            quantise_x(0)
+            w_mx.append(quantise(w_bf16[:], const, "w"))
+            transpose_kq(1, 1)
+            side_scores(0)
+            side_decay(0)
+            apply_decay(2)
+            scores(2 + AHEAD)
+            project_values(0, 0)
+            project_values(0, 1)
+            apply_decay(3)
+            scores(3 + AHEAD)
+            project_values(0, 2)
+            project_values(0, 3)
+            apply_decay(4)
+            scores(4 + AHEAD)
+            transpose_x(1, 0)
+            transpose_x(1, 1)
+
         def slot(s):
             b, odd = divmod(s, 2)
             u = len(USES) * s
@@ -324,64 +370,64 @@ def tile_multiscaleretention_pa_t_kernel(tc, q, k, x, W_v, out):
             scores(u + AHEAD)
             transpose_kq(s + 1, 0)
             if s == 1:
+                quantise_attn(0)
+                quantise_v(0)
                 quantise_x(1)
-            if odd:
+            elif odd:
                 quantise_v(b)
-            elif s > 0:
+                quantise_attn(s - 1)
+            else:
                 quantise_x(b + 1)
-            quantise_attn(s - 1)
+                quantise_attn(s - 1)
             side_scores(s)
             side_decay(s)
             transpose_kq(s + 1, 1)
             vb, vh = divmod(s + 1, 2)
-            if s == 0:
-                vb, vh = 0, 1
-            project_values(vb, 2 * vh)
-            if s == 0:
-                transpose_x(1, 0)
-                transpose_x(1, 1)
-            elif s == 1:
+            if s == 1:
                 transpose_x(2, 0)
                 transpose_x(2, 1)
             else:
                 transpose_x(b + 2, odd)
             apply_decay(u + 1)
             scores(u + 1 + AHEAD)
-            project_values(vb, 2 * vh + 1)
+            project_values(vb, 2 * vh)
             apply_decay(u + 2)
             scores(u + 2 + AHEAD)
-            output(s - 1, 0)
+            project_values(vb, 2 * vh + 1)
             apply_decay(u + 3)
             scores(u + 3 + AHEAD)
             if last:
                 first = quantise_part(s, 0, 0, BLOCKS)
-            output(s - 1, 1)
+            output(s - 1, 0)
             apply_decay(u + 4)
             scores(u + 4 + AHEAD)
+            output(s - 1, 1)
             if last:
                 second = quantise_part(s, 1, 0, 2)
                 third = quantise_part(s, 1, 2, BLOCKS)
                 output_part(s, 0, 0, BLOCKS, first, nc.scalar.copy)
                 output_part(s, 1, 0, 2, second, nc.vector.tensor_copy)
-                output_part(s, 1, 2, BLOCKS, third, nc.scalar.copy)
+                output_part(s, 1, 2, BLOCKS, third, nc.vector.tensor_copy)
 
+        for n in range(WARM_UP):
+            warm_ps = psum_vector.tile([P, TOKENS], F32, name="warm_ps", tag="bank")
+            nc.tensor.matmul(out=warm_ps[:], lhsT=zeros[:, 0:P], rhs=zeros[:], start=True, stop=True)
+        make_decay(0)
+        transpose_kq(0, 0)
+        transpose_kq(0, 1)
+        make_decay(1)
         w_bf16 = new_grouped(const, "w_bf16")
         x_bf16[0] = new_grouped(per_batch, "x_bf16")
-        for rows, grouped in ((x_sb[0], x_bf16[0]), (w_sb, w_bf16)):
-            for half, copy in enumerate((nc.scalar.copy, nc.vector.tensor_copy)):
-                copy_pairs(copy, transpose_pairs(rows, half), grouped, half)
-        make_decay(0)
-        make_decay(1)
-        transpose_kq(0, 0)
-        quantise_x(0)
-        w_mx.append(quantise(w_bf16[:], const, "w"))
-        transpose_kq(0, 1)
+        first_banks = [transpose_pairs(x_sb[0], half) for half in range(2)]
+        copy_pairs(nc.scalar.copy, first_banks[0], x_bf16[0], 0)
+        for u in range(AHEAD):
+            scores(u)
+        first_banks.extend(transpose_pairs(w_sb, half) for half in range(2))
+        copy_pairs(nc.scalar.copy, first_banks[2], w_bf16, 0)
+        load_batch(2)
+        load_x(3)
         make_decay(2)
         make_decay(3)
-        scores(0)
-        scores(1)
-        scores(2)
-        project_values(0, 0)
-        project_values(0, 1)
-        for s in range(SLOTS):
+        first_slot()
+        for s in range(1, SLOTS):
             slot(s)

@@ -19,7 +19,7 @@ BLOCKS = TOKENS // P
 SLOTS = BATCH * HEADS // 2
 FAR = 2.0**20
 
-WARM_UP = 4
+WARM_UP = 3
 
 FLOPS = 3 * 2 * BATCH * TOKENS * TOKENS * CHANNELS
 
@@ -55,11 +55,8 @@ def tile_multiscaleretention_pa_t_kernel(tc, q, k, x, W_v, out):
                 in_=matrix[:, columns].rearrange("(r p) c -> p r c", p=P),
             )
 
-        def load_half(rows, matrix, half):
-            nc.sync.dma_start(
-                out=rows[:, 2 * half : 2 * half + 2, :],
-                in_=matrix[pair_block(half), :].rearrange("(r p) c -> p r c", p=P),
-            )
+        def load_whole(rows, matrix):
+            nc.sync.dma_start(out=rows[:], in_=matrix.rearrange("(p r) c -> p r c", r=BLOCKS))
 
         every = slice(0, CHANNELS)
 
@@ -72,16 +69,15 @@ def tile_multiscaleretention_pa_t_kernel(tc, q, k, x, W_v, out):
         def load_x(b):
             if b < BATCH:
                 x_sb[b] = new_rows(inputs, "x_sb")
-                load(x_sb[b], x[b], every)
+                load_whole(x_sb[b], x[b])
 
         for store, name in ((k_sb, "k_sb"), (q_sb, "q_sb"), (x_sb, "x_sb")):
             store[0] = new_rows(inputs, name)
         w_sb = new_rows(const, "w_sb")
         load(k_sb[0], k[0], pair_block(0))
         load(q_sb[0], q[0], pair_block(0))
-        load_half(x_sb[0], x[0], 0)
-        load_half(x_sb[0], x[0], 1)
-        load(w_sb, W_v, every)
+        load_whole(x_sb[0], x[0])
+        load_whole(w_sb, W_v)
         load(k_sb[0], k[0], pair_block(1))
         load(q_sb[0], q[0], pair_block(1))
         load_x(1)
@@ -96,8 +92,6 @@ def tile_multiscaleretention_pa_t_kernel(tc, q, k, x, W_v, out):
             channel_multiplier=-1,
             allow_small_or_imprecise_dtypes=True,
         )
-        zeros = const.tile([P, TOKENS], BF16, name="zeros")
-        nc.vector.memset(zeros[:].bitcast(F32), 0.0)
         idents = []
         for name, dtype in (("ident_bf16", BF16), ("ident_f32", F32)):
             ident = const.tile([P, P], dtype, name=name)
@@ -127,6 +121,8 @@ def tile_multiscaleretention_pa_t_kernel(tc, q, k, x, W_v, out):
             nc.vector.memset(above[:, :, 0 : 2 * P * (BLOCKS - 1)], 0.0)
             attn_bf16.append(zeroed)
 
+        zeros = const.tile([P, TOKENS], BF16, name="zeros")
+        nc.vector.memset(zeros[:].bitcast(F32), 0.0)
         decay = const.tile([P, HEADS, P, BLOCKS], F32, name="decay")
 
         def make_decay(h):
@@ -157,10 +153,10 @@ def tile_multiscaleretention_pa_t_kernel(tc, q, k, x, W_v, out):
             return bank
 
         def copy_pairs(copy, bank, grouped, half):
-            pairs = grouped[:].bitcast(F32).rearrange("p (n u) -> p n u", u=2)
+            pairs = grouped[:].bitcast(F32).rearrange("p (t r u) -> p t r u", r=BLOCKS, u=2)
             copy(
-                out=pairs[:, 2 * P * half : 2 * P * (half + 1), :],
-                in_=bank[:].rearrange("p u n -> p n u"),
+                out=pairs[:, :, 2 * half : 2 * half + 2, :],
+                in_=bank[:].rearrange("p u (r t) -> p t r u", r=2),
             )
 
         x_bf16, x_mx, v_bf16, v_mx = {}, {}, {}, {}
@@ -336,11 +332,9 @@ def tile_multiscaleretention_pa_t_kernel(tc, q, k, x, W_v, out):
         def first_slot():
             apply_decay(0)
             scores(AHEAD)
-            copy_pairs(nc.vector.tensor_copy, first_banks[1], x_bf16[0], 1)
             transpose_kq(1, 0)
             apply_decay(1)
             scores(1 + AHEAD)
-            copy_pairs(nc.vector.tensor_copy, first_banks[3], w_bf16, 1)
             quantise_x(0)
             w_mx.append(quantise(w_bf16[:], const, "w"))
             transpose_kq(1, 1)
@@ -353,9 +347,9 @@ def tile_multiscaleretention_pa_t_kernel(tc, q, k, x, W_v, out):
             apply_decay(3)
             scores(3 + AHEAD)
             project_values(0, 2)
-            project_values(0, 3)
             apply_decay(4)
             scores(4 + AHEAD)
+            project_values(0, 3, nc.vector.tensor_copy)
             transpose_x(1, 0)
             transpose_x(1, 1)
 
@@ -368,6 +362,7 @@ def tile_multiscaleretention_pa_t_kernel(tc, q, k, x, W_v, out):
                 load_x(b + 3)
             apply_decay(u)
             scores(u + AHEAD)
+            side_scores(s)
             transpose_kq(s + 1, 0)
             if s == 1:
                 quantise_attn(0)
@@ -379,7 +374,6 @@ def tile_multiscaleretention_pa_t_kernel(tc, q, k, x, W_v, out):
             else:
                 quantise_x(b + 1)
                 quantise_attn(s - 1)
-            side_scores(s)
             side_decay(s)
             transpose_kq(s + 1, 1)
             vb, vh = divmod(s + 1, 2)
@@ -395,10 +389,10 @@ def tile_multiscaleretention_pa_t_kernel(tc, q, k, x, W_v, out):
             scores(u + 2 + AHEAD)
             project_values(vb, 2 * vh + 1)
             apply_decay(u + 3)
-            scores(u + 3 + AHEAD)
             if last:
                 first = quantise_part(s, 0, 0, BLOCKS)
             output(s - 1, 0)
+            scores(u + 3 + AHEAD)
             apply_decay(u + 4)
             scores(u + 4 + AHEAD)
             output(s - 1, 1)
@@ -412,22 +406,20 @@ def tile_multiscaleretention_pa_t_kernel(tc, q, k, x, W_v, out):
         for n in range(WARM_UP):
             warm_ps = psum_vector.tile([P, TOKENS], F32, name="warm_ps", tag="bank")
             nc.tensor.matmul(out=warm_ps[:], lhsT=zeros[:, 0:P], rhs=zeros[:], start=True, stop=True)
-        make_decay(0)
+        for h in range(4):
+            make_decay(h)
         transpose_kq(0, 0)
         transpose_kq(0, 1)
-        make_decay(1)
         w_bf16 = new_grouped(const, "w_bf16")
         x_bf16[0] = new_grouped(per_batch, "x_bf16")
-        first_banks = [transpose_pairs(x_sb[0], half) for half in range(2)]
-        copy_pairs(nc.scalar.copy, first_banks[0], x_bf16[0], 0)
+        for half in range(2):
+            copy_pairs(nc.scalar.copy, transpose_pairs(x_sb[0], half), x_bf16[0], half)
         for u in range(AHEAD):
             scores(u)
-        first_banks.extend(transpose_pairs(w_sb, half) for half in range(2))
-        copy_pairs(nc.scalar.copy, first_banks[2], w_bf16, 0)
+        for half in range(2):
+            copy_pairs(nc.scalar.copy, transpose_pairs(w_sb, half), w_bf16, half)
         load_batch(2)
         load_x(3)
-        make_decay(2)
-        make_decay(3)
         first_slot()
         for s in range(1, SLOTS):
             slot(s)

@@ -92,6 +92,14 @@ def tile_multiscaleretention_pa_t_kernel(tc, q, k, x, W_v, out):
             channel_multiplier=-1,
             allow_small_or_imprecise_dtypes=True,
         )
+        attn_bf16 = []
+        def zeroed_tile(engine, n):
+            tile = const.tile([P, 2, TOKENS, PACK], BF16, name="attn_bf16_%d" % n, align_bytes=64)
+            above = tile[:].rearrange("p n t j -> p n (t j)").bitcast(F32)
+            engine.memset(above[:, :, 0 : 2 * P * (BLOCKS - 1)], 0.0)
+            attn_bf16.append(tile)
+
+        zeroed_tile(nc.vector, 0)
         idents = []
         for name, dtype in (("ident_bf16", BF16), ("ident_f32", F32)):
             ident = const.tile([P, P], dtype, name=name)
@@ -104,6 +112,8 @@ def tile_multiscaleretention_pa_t_kernel(tc, q, k, x, W_v, out):
             )
             idents.append(ident)
         ident_bf16, ident_f32 = idents
+        zeros = const.tile([P, TOKENS], BF16, name="zeros")
+        nc.vector.memset(zeros[:].bitcast(F32), 0.0)
         nc.gpsimd.affine_select(
             out=distance[:, :, BLOCKS - 1],
             in_=distance[:, :, BLOCKS - 1],
@@ -114,15 +124,8 @@ def tile_multiscaleretention_pa_t_kernel(tc, q, k, x, W_v, out):
             channel_multiplier=-1,
         )
 
-        attn_bf16 = []
-        for n in range(2):
-            zeroed = const.tile([P, 2, TOKENS, PACK], BF16, name="attn_bf16_%d" % n, align_bytes=64)
-            above = zeroed[:].rearrange("p n t j -> p n (t j)").bitcast(F32)
-            nc.vector.memset(above[:, :, 0 : 2 * P * (BLOCKS - 1)], 0.0)
-            attn_bf16.append(zeroed)
+        zeroed_tile(nc.gpsimd, 1)
 
-        zeros = const.tile([P, TOKENS], BF16, name="zeros")
-        nc.vector.memset(zeros[:].bitcast(F32), 0.0)
         decay = const.tile([P, HEADS, P, BLOCKS], F32, name="decay")
 
         def make_decay(h):
@@ -377,11 +380,9 @@ def tile_multiscaleretention_pa_t_kernel(tc, q, k, x, W_v, out):
             side_decay(s)
             transpose_kq(s + 1, 1)
             vb, vh = divmod(s + 1, 2)
-            if s == 1:
-                transpose_x(2, 0)
-                transpose_x(2, 1)
-            else:
-                transpose_x(b + 2, odd)
+            if odd:
+                transpose_x(b + 2, 0)
+                transpose_x(b + 2, 1)
             apply_decay(u + 1)
             scores(u + 1 + AHEAD)
             project_values(vb, 2 * vh)

@@ -36,7 +36,8 @@ def tile_multiscaleretention_pa_t_kernel(tc, q, k, x, W_v, out):
     nc = tc.nc
     with ExitStack() as ctx:
         const = ctx.enter_context(tc.tile_pool(name="const", bufs=1))
-        inputs = ctx.enter_context(tc.tile_pool(name="inputs", bufs=BATCH))
+        inputs = ctx.enter_context(tc.tile_pool(name="inputs", bufs=3))
+        every_slot = ctx.enter_context(tc.tile_pool(name="every_slot", bufs=SLOTS))
         per_batch = ctx.enter_context(tc.tile_pool(name="per_batch", bufs=2))
         per_slot = ctx.enter_context(tc.tile_pool(name="per_slot", bufs=3))
         transposed = ctx.enter_context(tc.tile_pool(name="transposed", bufs=6))
@@ -259,7 +260,7 @@ def tile_multiscaleretention_pa_t_kernel(tc, q, k, x, W_v, out):
             bank = psum_scalar.tile([P, 4, P], F32, name="side_ps", tag="bank")
             for place, (n, i, j) in enumerate(((0, 0, 0), (1, 0, 0), (1, 1, 0), (1, 1, 1))):
                 score_block(bank[:, place, :], s, n, i, j)
-            side_sb[s] = per_slot.tile([P, 4, P], F32, name="side_sb")
+            side_sb[s] = every_slot.tile([P, 4, P], F32, name="side_sb")
             nc.scalar.copy(out=side_sb[s][:], in_=bank[:])
 
         def side_decay(s):
@@ -301,7 +302,7 @@ def tile_multiscaleretention_pa_t_kernel(tc, q, k, x, W_v, out):
                 return
             b, h = s // 2, 2 * (s % 2)
             if n == 0:
-                y_sb[s] = per_slot.tile([P, BLOCKS, 2, P], F32, name="y_sb")
+                y_sb[s] = every_slot.tile([P, BLOCKS, 2, P], F32, name="y_sb")
             y_ps = psum_scalar.tile([P, BLOCKS, P], F32, name="y_ps", tag="bank")
             for i in range(BLOCKS):
                 at = block(BLOCKS * n + i)

import math
from contextlib import ExitStack

import concourse.mybir as mybir

F32 = mybir.dt.float32
BF16 = mybir.dt.bfloat16
U32 = mybir.dt.uint32
U8 = mybir.dt.uint8
FP8X4 = mybir.dt.float8_e4m3fn_x4

P = 128
PACK = 4
BATCH = 8
TOKENS = 512
CHANNELS = 512
HEADS = CHANNELS // P
BLOCKS = TOKENS // P
SLOTS = BATCH * HEADS // 2
FAR = 2.0**20

WARM_UP = 3

FLOPS = 3 * 2 * BATCH * TOKENS * TOKENS * CHANNELS


def block(n):
    return slice(P * n, P * (n + 1))


def pair_block(n):
    return slice(2 * P * n, 2 * P * (n + 1))


def tile_multiscaleretention_pa_t_kernel(tc, q, k, x, W_v, out):
    nc = tc.nc
    with ExitStack() as ctx:
        const = ctx.enter_context(tc.tile_pool(name="const", bufs=1))
        inputs = ctx.enter_context(tc.tile_pool(name="inputs", bufs=3))
        every_slot = ctx.enter_context(tc.tile_pool(name="every_slot", bufs=SLOTS))
        per_batch = ctx.enter_context(tc.tile_pool(name="per_batch", bufs=2))
        per_slot = ctx.enter_context(tc.tile_pool(name="per_slot", bufs=3))
        transposed = ctx.enter_context(tc.tile_pool(name="transposed", bufs=6))
        psum_scalar = ctx.enter_context(tc.psum_pool(name="psum_scalar", bufs=4))
        psum_vector = ctx.enter_context(tc.psum_pool(name="psum_vector", bufs=4))
        ctx.enter_context(tc.manual_schedule())

        k_sb, q_sb, x_sb = {}, {}, {}

        def new_rows(pool, name):
            return pool.tile([P, BLOCKS, CHANNELS], BF16, name=name, tag=name)

        def load(rows, matrix, columns):
            nc.sync.dma_start(
                out=rows[:, :, columns],
                in_=matrix[:, columns].rearrange("(r p) c -> p r c", p=P),
            )

        def load_whole(rows, matrix):
            nc.sync.dma_start(out=rows[:], in_=matrix.rearrange("(p r) c -> p r c", r=BLOCKS))

        every = slice(0, CHANNELS)

        def load_batch(b):
            if b < BATCH:
                for store, matrix, name in ((k_sb, k, "k_sb"), (q_sb, q, "q_sb")):
                    store[b] = new_rows(inputs, name)
                    load(store[b], matrix[b], every)

        def load_x(b):
            if b < BATCH:
                x_sb[b] = new_rows(inputs, "x_sb")
                load_whole(x_sb[b], x[b])

        for store, name in ((k_sb, "k_sb"), (q_sb, "q_sb"), (x_sb, "x_sb")):
            store[0] = new_rows(inputs, name)
        w_sb = new_rows(const, "w_sb")
        load(k_sb[0], k[0], pair_block(0))
        load(q_sb[0], q[0], pair_block(0))
        load_whole(x_sb[0], x[0])
        load_whole(w_sb, W_v)
        load(k_sb[0], k[0], pair_block(1))
        load(q_sb[0], q[0], pair_block(1))
        load_x(1)
        load_batch(1)
        load_x(2)

        distance = const.tile([P, P, BLOCKS], F32, name="distance")
        nc.gpsimd.iota(
            distance[:],
            pattern=[[1, P], [-P, BLOCKS]],
            base=P * (BLOCKS - 1),
            channel_multiplier=-1,
            allow_small_or_imprecise_dtypes=True,
        )
        attn_bf16 = []
        def zeroed_tile(engine, n):
            tile = const.tile([P, 2, TOKENS, PACK], BF16, name="attn_bf16_%d" % n, align_bytes=64)
            above = tile[:].rearrange("p n t j -> p n (t j)").bitcast(F32)
            engine.memset(above[:, :, 0 : 2 * P * (BLOCKS - 1)], 0.0)
            attn_bf16.append(tile)

        zeroed_tile(nc.vector, 0)
        idents = []
        for name, dtype in (("ident_bf16", BF16), ("ident_f32", F32)):
            ident = const.tile([P, P], dtype, name=name)
            nc.vector.tensor_scalar(
                out=ident[:],
                in0=distance[:, :, BLOCKS - 1],
                scalar1=0.0,
                scalar2=None,
                op0=mybir.AluOpType.is_equal,
            )
            idents.append(ident)
        ident_bf16, ident_f32 = idents
        zeros = const.tile([P, TOKENS], BF16, name="zeros")
        nc.vector.memset(zeros[:].bitcast(F32), 0.0)
        nc.gpsimd.affine_select(
            out=distance[:, :, BLOCKS - 1],
            in_=distance[:, :, BLOCKS - 1],
            compare_op=mybir.AluOpType.is_ge,
            fill=FAR,
            pattern=[[1, P]],
            base=0,
            channel_multiplier=-1,
        )

        zeroed_tile(nc.gpsimd, 1)

        decay = const.tile([P, HEADS, P, BLOCKS], F32, name="decay")

        def make_decay(h):
            nc.scalar.activation(
                out=decay[:, h],
                in_=distance[:],
                func=mybir.ActivationFunctionType.Exp,
                scale=math.log(1.0 - 2.0 ** (-5 - h)),
                bias=-0.5 * math.log(P),
            )

        def quantise(grouped, pool, name):
            n = grouped.shape[1] // PACK
            words = pool.tile([P, n], U32, name=name + "_words", align_bytes=64)
            scales = pool.tile([P, n], U8, name=name + "_scales", align_bytes=64)
            nc.vector.quantize_mx(out=words[:].bitcast(FP8X4), scales=scales[:], in_=grouped)
            return words, scales

        def new_grouped(pool, name):
            return pool.tile([P, TOKENS * PACK], BF16, name=name, align_bytes=64)

        def transpose_pairs(rows, half):
            bank = psum_scalar.tile([P, 2, 2 * P], F32, name="pairs_ps", tag="bank")
            for n in range(2):
                row_pairs = rows[:, 2 * half + n, :].bitcast(F32)
                for u in range(2):
                    nc.tensor.transpose(bank[:, u, block(n)], row_pairs[:, block(u)], ident_f32[:])
            return bank

        def copy_pairs(copy, bank, grouped, half):
            pairs = grouped[:].bitcast(F32).rearrange("p (t r u) -> p t r u", r=BLOCKS, u=2)
            copy(
                out=pairs[:, :, 2 * half : 2 * half + 2, :],
                in_=bank[:].rearrange("p u (r t) -> p t r u", r=2),
            )

        x_bf16, x_mx, v_bf16, v_mx = {}, {}, {}, {}

        x_banks = {}

        def transpose_x(b, half, copy=nc.scalar.copy):
            if b >= BATCH:
                return
            if half == 0:
                x_bf16[b] = new_grouped(per_batch, "x_bf16")
            x_banks[b, half] = transpose_pairs(x_sb[b], half)
            if copy:
                copy_x(copy, b, half)

        def copy_x(copy, b, half):
            if b < BATCH:
                copy_pairs(copy, x_banks[b, half], x_bf16[b], half)

        def quantise_x(b):
            if b < BATCH:
                x_mx[b] = quantise(x_bf16[b][:], per_batch, "x")

        def project_values(b, h, copy=nc.scalar.copy):
            if b >= BATCH:
                return
            v_ps = psum_scalar.tile([P, BLOCKS, P], F32, name="v_ps", tag="bank")
            for j in range(BLOCKS):
                nc.tensor.matmul_mx(
                    out=v_ps[:, j, :],
                    lhsT=x_mx[b][0][:, block(j)].bitcast(FP8X4),
                    lhsT_scale=x_mx[b][1][:, block(j)],
                    rhs=w_mx[0][0][:, block(h)].bitcast(FP8X4),
                    rhs_scale=w_mx[0][1][:, block(h)],
                    start=True,
                    stop=True,
                )
            if h == 0:
                v_bf16[b] = per_batch.tile([P, HEADS, P, PACK], BF16, name="v_bf16", align_bytes=64)
            copy(out=v_bf16[b][:, h], in_=v_ps[:].rearrange("p j c -> p c j"))

        def quantise_v(b):
            v_mx[b] = quantise(v_bf16[b][:].rearrange("p h c j -> p (h c j)"), per_batch, "v")

        kq, s_ps, side_sb, a_mx = {}, {}, {}, {}

        def transpose_kq(s, n):
            if s >= SLOTS:
                return
            b, h = s // 2, 2 * (s % 2) + n
            kq_ps = psum_scalar.tile([P, 2, TOKENS], BF16, name="kq_ps", tag="bank")
            for side, rows in enumerate((k_sb[b], q_sb[b])):
                for i in range(BLOCKS):
                    nc.tensor.matmul(
                        out=kq_ps[:, side, block(i)],
                        lhsT=rows[:, i, block(h)],
                        rhs=ident_bf16[:],
                        start=True,
                        stop=True,
                    )
            kq[s, n] = transposed.tile([P, 2, TOKENS], BF16, name="kq")
            nc.scalar.copy(out=kq[s, n][:], in_=kq_ps[:])

        def score_block(bank, s, n, i, j):
            nc.tensor.matmul(
                out=bank,
                lhsT=kq[s, n][:, 0, block(j)],
                rhs=kq[s, n][:, 1, block(i)],
                start=True,
                stop=True,
            )

        USES = ((2, 0), (3, 0), (1, 0), (2, 1), (3, 1))

        def scores(u):
            s, use = divmod(u, len(USES))
            if s >= SLOTS:
                return
            i, n = USES[use]
            s_ps[u] = psum_vector.tile([P, BLOCKS, P], F32, name="s_ps", tag="bank")
            for j in range(i + 1):
                score_block(s_ps[u][:, j, :], s, n, i, j)

        def apply_decay(u):
            s, use = divmod(u, len(USES))
            i, n = USES[use]
            nc.vector.tensor_tensor(
                out=attn_bf16[s % 2][:, n, block(i), 0 : i + 1],
                in0=s_ps[u][:, 0 : i + 1, :].rearrange("p j t -> p t j"),
                in1=decay[:, 2 * (s % 2) + n, :, BLOCKS - 1 - i : BLOCKS],
                op=mybir.AluOpType.mult,
            )

        def side_scores(s):
            if s >= SLOTS:
                return
            bank = psum_scalar.tile([P, 4, P], F32, name="side_ps", tag="bank")
            for place, (n, i, j) in enumerate(((0, 0, 0), (1, 0, 0), (1, 1, 0), (1, 1, 1))):
                score_block(bank[:, place, :], s, n, i, j)
            side_sb[s] = every_slot.tile([P, 4, P], F32, name="side_sb")
            nc.scalar.copy(out=side_sb[s][:], in_=bank[:])

        def side_decay(s):
            if s >= SLOTS:
                return
            h = 2 * (s % 2)
            nc.gpsimd.tensor_tensor(
                out=attn_bf16[s % 2][:, :, block(0), 0],
                in0=side_sb[s][:, 0:2, :],
                in1=decay[:, h : h + 2, :, BLOCKS - 1],
                op=mybir.AluOpType.mult,
            )
            nc.gpsimd.tensor_tensor(
                out=attn_bf16[s % 2][:, 1, block(1), 0:2],
                in0=side_sb[s][:, 2:4, :].rearrange("p j t -> p t j"),
                in1=decay[:, h + 1, :, BLOCKS - 2 : BLOCKS],
                op=mybir.AluOpType.mult,
            )

        def quantise_attn(s):
            if s >= 0:
                a_mx[s] = quantise(attn_bf16[s % 2][:].rearrange("p n t j -> p (n t j)"), per_slot, "a")

        def attend(out_, words, scales, b, h):
            nc.tensor.matmul_mx(
                out=out_,
                lhsT=words.bitcast(FP8X4),
                lhsT_scale=scales,
                rhs=v_mx[b][0][:, block(h)].bitcast(FP8X4),
                rhs_scale=v_mx[b][1][:, block(h)],
                start=True,
                stop=True,
            )

        y_sb = {}

        def output(s, n):
            if s < 0:
                return
            b, h = s // 2, 2 * (s % 2)
            if n == 0:
                y_sb[s] = every_slot.tile([P, BLOCKS, 2, P], F32, name="y_sb")
            y_ps = psum_scalar.tile([P, BLOCKS, P], F32, name="y_ps", tag="bank")
            for i in range(BLOCKS):
                at = block(BLOCKS * n + i)
                attend(y_ps[:, i, :], a_mx[s][0][:, at], a_mx[s][1][:, at], b, h + n)
            nc.scalar.copy(out=y_sb[s][:, :, n, :], in_=y_ps[:])
            if n == 1:
                nc.sync.dma_start(
                    out=out[b][:, pair_block(s % 2)].rearrange("(i p) (n c) -> p i n c", p=P, n=2),
                    in_=y_sb[s][:],
                )

        def quantise_part(s, n, i0, i1):
            part = attn_bf16[s % 2][:, n, P * i0 : P * i1, :].rearrange("p t j -> p (t j)")
            return quantise(part, const, "last_%d_%d" % (n, i0))

        def output_part(s, n, i0, i1, part, copy):
            b, h = s // 2, 2 * (s % 2) + n
            last_y = const.tile([P, i1 - i0, P], F32, name="last_y_%d_%d" % (n, i0))
            y_ps = psum_scalar.tile([P, i1 - i0, P], F32, name="y_ps", tag="bank")
            for i in range(i1 - i0):
                attend(y_ps[:, i, :], part[0][:, block(i)], part[1][:, block(i)], b, h)
            copy(out=last_y[:], in_=y_ps[:])
            nc.sync.dma_start(
                out=out[b][P * i0 : P * i1, block(h)].rearrange("(i p) c -> p i c", p=P), in_=last_y[:]
            )

        w_mx = []

        AHEAD = 3

        def first_slot():
            apply_decay(0)
            scores(AHEAD)
            transpose_kq(1, 0)
            apply_decay(1)
            scores(1 + AHEAD)
            quantise_x(0)
            w_mx.append(quantise(w_bf16[:], const, "w"))
            transpose_kq(1, 1)
            side_scores(0)
            side_decay(0)
            apply_decay(2)
            scores(2 + AHEAD)
            project_values(0, 0)
            project_values(0, 1)
            apply_decay(3)
            scores(3 + AHEAD)
            project_values(0, 2)
            apply_decay(4)
            scores(4 + AHEAD)
            project_values(0, 3, nc.vector.tensor_copy)
            transpose_x(1, 0)
            transpose_x(1, 1)

        def slot(s):
            b, odd = divmod(s, 2)
            u = len(USES) * s
            last = s == SLOTS - 1
            if not odd:
                load_batch(b + 2)
                load_x(b + 3)
            apply_decay(u)
            scores(u + AHEAD)
            side_scores(s)
            transpose_kq(s + 1, 0)
            if s == 1:
                quantise_attn(0)
                quantise_v(0)
                quantise_x(1)
            elif odd:
                quantise_v(b)
                quantise_attn(s - 1)
            else:
                quantise_x(b + 1)
                quantise_attn(s - 1)
            side_decay(s)
            transpose_kq(s + 1, 1)
            vb, vh = divmod(s + 1, 2)
            if odd:
                transpose_x(b + 2, 0)
                transpose_x(b + 2, 1)
            apply_decay(u + 1)
            scores(u + 1 + AHEAD)
            project_values(vb, 2 * vh)
            apply_decay(u + 2)
            scores(u + 2 + AHEAD)
            project_values(vb, 2 * vh + 1)
            apply_decay(u + 3)
            if last:
                first = quantise_part(s, 0, 0, BLOCKS)
            output(s - 1, 0)
            scores(u + 3 + AHEAD)
            apply_decay(u + 4)
            scores(u + 4 + AHEAD)
            output(s - 1, 1)
            if last:
                second = quantise_part(s, 1, 0, 2)
                third = quantise_part(s, 1, 2, BLOCKS)
                output_part(s, 0, 0, BLOCKS, first, nc.scalar.copy)
                output_part(s, 1, 0, 2, second, nc.vector.tensor_copy)
                output_part(s, 1, 2, BLOCKS, third, nc.vector.tensor_copy)

        for n in range(WARM_UP):
            warm_ps = psum_vector.tile([P, TOKENS], F32, name="warm_ps", tag="bank")
            nc.tensor.matmul(out=warm_ps[:], lhsT=zeros[:, 0:P], rhs=zeros[:], start=True, stop=True)
        for h in range(4):
            make_decay(h)
        transpose_kq(0, 0)
        transpose_kq(0, 1)
        w_bf16 = new_grouped(const, "w_bf16")
        x_bf16[0] = new_grouped(per_batch, "x_bf16")
        for half in range(2):
            copy_pairs(nc.scalar.copy, transpose_pairs(x_sb[0], half), x_bf16[0], half)
        for u in range(AHEAD):
            scores(u)
        for half in range(2):
            copy_pairs(nc.scalar.copy, transpose_pairs(w_sb, half), w_bf16, half)
        load_batch(2)
        load_x(3)
        first_slot()
        for s in range(1, SLOTS):
            slot(s)
